import numpy as np
import ml_dtypes


def mxq(x, axis, fmt="e4m3"):
    dtype, down = {"e4m3": (ml_dtypes.float8_e4m3fn, 7), "e5m2": (ml_dtypes.float8_e5m2, 14)}[fmt]
    v = np.moveaxis(np.asarray(x, np.float32).astype(ml_dtypes.bfloat16).astype(np.float64), axis, -1)
    blocks = v.reshape(v.shape[:-1] + (-1, 32))
    amax = np.abs(blocks).max(-1, keepdims=True)
    byte = np.maximum(np.where(amax > 0, np.frexp(amax)[1] - 1 + 127, 0) - down, 1)
    scale = np.exp2(byte - 127.0)
    codes = (blocks / scale).astype(np.float32).astype(dtype).astype(np.float64)
    return np.moveaxis((codes * scale).reshape(v.shape), -1, axis)


WIDE = False


def mx_kscale(k):
    if not WIDE:
        return np.ones(k)
    levels = np.array([10, -10, 5, -5, 0])
    a = np.random.permutation(np.resize(levels, k // 512 * 4)).reshape(k // 512, 4)
    idx = np.arange(k)
    return np.exp2(a[idx // 512, idx % 128 // 32])


BF16 = ml_dtypes.bfloat16


def bf(x):
    return np.asarray(x, np.float32).astype(BF16)


def f64(x):
    return np.asarray(x).astype(np.float64)


B, H, W, C, U, K = 8, 35, 35, 64, 512, 4
D = K * K * C
P_SCALE = 5.0
Q_SCALE = 0.3
EPS = 1e-6
L2_EPS = 1e-12


def im2col_valid(x, k):
    nb, nh, nw, nc_ = x.shape
    oy, ox = nh - k + 1, nw - k + 1
    patches = np.stack([x[:, i:i + oy, j:j + ox, :] for i in range(k) for j in range(k)], axis=3)
    return patches.reshape(nb, oy * ox, k * k * nc_), oy, ox


def chan_scale():
    blk = np.sort(mx_kscale(D)[::32])
    pick = np.round(np.linspace(0, len(blk) - 1, C // 32)).astype(int)
    return np.repeat(blk[pick], 32)


def setup_inputs():
    sc = chan_scale()
    s = np.tile(sc, K * K)
    g = np.random.uniform(0.5, 1.5, (1, 1, U)) * np.sign(np.random.standard_normal((1, 1, U)))
    return {"x": bf(np.abs(np.random.standard_normal((B, H, W, C))) * 0.25 * sc),
            "w": bf((np.random.standard_normal((1, D, U)) + g) * 2.0 / np.sqrt(D) / s[None, :, None]),
            "p": bf(0.7 * P_SCALE * (1.0 + 0.1 * np.random.standard_normal(U))),
            "q": bf(0.2 * (1.0 + 0.1 * np.random.standard_normal(1)))}


def reference(x, w, p, q):
    x, w, p, q = f64(x), f64(w), f64(p), f64(q)
    nb = x.shape[0]
    patches, oy, ox = im2col_valid(x, K)
    qq = np.square(q / Q_SCALE)
    x_norm = np.sqrt(np.maximum(np.sum(np.square(patches), axis=2, keepdims=True), L2_EPS)) + qq
    w_norm = np.sqrt(np.maximum(np.sum(np.square(w), axis=1, keepdims=True), L2_EPS)) + qq
    sim = mxq(patches / x_norm, 2, "e4m3") @ mxq(w / w_norm, 1, "e4m3")
    sign = np.sign(sim)
    out = sign * np.power(np.abs(sim) + EPS, np.square(p / P_SCALE))
    return out.reshape(nb, oy, ox, w.shape[2])

@@ -1,0 +1,296 @@
+from contextlib import ExitStack
+
+import concourse.mybir as mybir
+from concourse.masks import make_identity
+
+F32 = mybir.dt.float32
+BF16 = mybir.dt.bfloat16
+U32 = mybir.dt.uint32
+U8 = mybir.dt.uint8
+FP8X4 = mybir.dt.float8_e4m3fn_x4
+ACT = mybir.ActivationFunctionType
+ALU = mybir.AluOpType
+AX = mybir.AxisListType
+
+FLOPS = 2 * 8192 * 1024 * 512
+
+P = 128
+ROW = 35 * 64
+NQ = 16
+MANUAL = True
+S_EXITS = (1, 3)
+CHUNKS = ((0, 1, 2, 3), (4, 5, 6, 7), (8, 9, 10, 11), (12, 13), (14, 15))
+
+
+def tile_cossim2d_t_kernel(tc, x, w, p, q, out):
+    nc = tc.nc
+    with ExitStack() as ctx:
+        const = ctx.enter_context(tc.tile_pool(name="const", bufs=1))
+        work = ctx.enter_context(tc.tile_pool(name="work", bufs=2))
+        epi = ctx.enter_context(tc.tile_pool(name="epi", bufs=8))
+        psum = ctx.enter_context(tc.psum_pool(name="psum", bufs=4))
+
+        x_rows = x.rearrange("b h w c -> (b h) (w c)")
+        xr = []
+        for k in range(3):
+            xr_k = epi.tile([P, ROW], BF16, tag="sg", name="xr%d" % k)
+            xr.append(xr_k)
+        nc.vector.memset(xr[2][:], 0.0)
+        nc.sync.dma_start(out=xr[0][:], in_=x_rows[0:128, :])
+        nc.sync.dma_start(out=xr[1][:], in_=x_rows[128:256, :])
+        nc.sync.dma_start(out=xr[2][0:24, :], in_=x_rows[256:280, :])
+
+        q_sb = const.tile([P, 1], BF16)
+        nc.scalar.dma_start(out=q_sb[:], in_=q.partition_broadcast(P))
+        w_raw = epi.tile([P, 8, 512], BF16, tag="big", align_bytes=64)
+        nc.scalar.dma_start(out=w_raw[:], in_=w.rearrange("o (s p) n -> p (o s) n", p=P))
+        p_bc = const.tile([P, 512], BF16)
+        nc.scalar.dma_start(out=p_bc[:], in_=p.partition_broadcast(P))
+
+        xs2 = const.tile([P, 8, ROW], BF16)
+        for h in range(2):
+            for i in (0, 2, 1, 3):
+                nc.sync.dma_start(
+                    out=xs2[32 * i : 32 * i + 32, 4 * h : 4 * h + 4, :],
+                    in_=x[4 * h : 4 * h + 4, i : i + 32, :, :].rearrange("b y w c -> y b (w c)"),
+                )
+
+        eps_t = const.tile([P, 1], F32)
+        nc.vector.memset(eps_t[:], 1e-6)
+        junk = const.tile([P, 1], F32)
+        nc.scalar.activation(out=junk[:], in_=eps_t[:], func=ACT.Sqrt)
+        ident_bf = const.tile([P, P], BF16)
+        make_identity(nc, ident_bf[:])
+        ident_f = const.tile([P, P], F32)
+        make_identity(nc, ident_f[:])
+        perm = const.tile([P, P], BF16)
+        nc.vector.tensor_copy(
+            out=perm[:].rearrange("p (y i) -> p y i", i=4),
+            in_=ident_bf[:].rearrange("p (i y) -> p y i", i=4),
+        )
+        ones_f = const.tile([P, P], F32)
+        nc.vector.memset(ones_f[:], 1.0)
+        iext = const.tile([P, 196], F32)
+        nc.vector.memset(iext[:], 0.0)
+        nc.vector.tensor_copy(out=iext[:, 32:160], in_=ident_f[:])
+        band = const.tile([P, 192], F32)
+        nc.vector.tensor_tensor(out=band[:], in0=iext[:, 0:192], in1=iext[:, 1:193], op=ALU.add)
+        nc.vector.tensor_tensor(out=band[:], in0=band[:], in1=iext[:, 2:194], op=ALU.add)
+        nc.vector.tensor_tensor(out=band[:], in0=band[:], in1=iext[:, 3:195], op=ALU.add)
+        pairs = ((0, 0), (1, 0), (2, 0), (3, 0), (3, 1), (4, 1), (5, 1), (6, 1), (7, 1), (7, 2))
+        sel = const.tile([P, 10, 4, 32], F32)
+        for idx, (b, k) in enumerate(pairs):
+            o = 32 + 35 * b - 128 * k
+            nc.vector.tensor_copy(
+                out=sel[:, idx, :, :],
+                in_=band[:, o : o + 32].unsqueeze(1).to_broadcast([P, 4, 32]),
+            )
+        qq = const.tile([P, 1], F32)
+        nc.scalar.activation(out=qq[:], in_=q_sb[:], func=ACT.Square, scale=1.0 / 0.3)
+
+        csum = const.tile([P, 3, 35], F32)
+        for k in range(3):
+            sq = epi.tile([P, ROW], F32, tag="big", align_bytes=64)
+            nc.scalar.activation(out=sq[:], in_=xr[k][:], func=ACT.Square)
+            nc.vector.tensor_reduce(
+                out=csum[:, k, :],
+                in_=sq[:].rearrange("p (w c) -> p w c", c=64),
+                axis=AX.X,
+                op=ALU.add,
+            )
+        rsum = const.tile([P, 3, 32], F32)
+        nc.vector.tensor_tensor(out=rsum[:], in0=csum[:, :, 0:32], in1=csum[:, :, 1:33], op=ALU.add)
+        nc.vector.tensor_tensor(out=rsum[:], in0=rsum[:], in1=csum[:, :, 2:34], op=ALU.add)
+        nc.vector.tensor_tensor(out=rsum[:], in0=rsum[:], in1=csum[:, :, 3:35], op=ALU.add)
+        ss = psum.tile([P, 256], F32, tag="acc")
+        for idx, (b, k) in enumerate(pairs):
+            first = idx == 0 or pairs[idx - 1][0] != b
+            last = idx == 9 or pairs[idx + 1][0] != b
+            nc.tensor.matmul(
+                out=ss[:, 32 * b : 32 * b + 32],
+                lhsT=sel[:, idx, :, :].rearrange("p i y -> p (i y)"),
+                rhs=rsum[:, k, :],
+                start=first,
+                stop=last,
+            )
+        xn = const.tile([P, 256], F32)
+        nc.vector.tensor_scalar(out=xn[:], in0=ss[:], scalar1=1e-12, scalar2=None, op0=ALU.max)
+        nc.scalar.activation(out=xn[:], in_=xn[:], func=ACT.Sqrt)
+        nc.vector.tensor_scalar(out=xn[:], in0=xn[:], scalar1=qq[:, 0:1], scalar2=None, op0=ALU.add)
+        rn = const.tile([P, 256], F32)
+        nc.vector.reciprocal(out=rn[:], in_=xn[:])
+
+        wss = psum.tile([P, 512], F32, tag="acc")
+        for hh in range(2):
+            wsq = epi.tile([P, 4, 512], F32, tag="big", align_bytes=64)
+            nc.scalar.activation(out=wsq[:], in_=w_raw[:, 4 * hh : 4 * hh + 4, :], func=ACT.Square)
+            for s in range(4):
+                nc.tensor.matmul(
+                    out=wss[:],
+                    lhsT=ones_f[:],
+                    rhs=wsq[:, s, :],
+                    start=(hh == 0 and s == 0),
+                    stop=(hh == 1 and s == 3),
+                )
+        wn = const.tile([P, 512], F32)
+        nc.vector.tensor_scalar(out=wn[:], in0=wss[:], scalar1=1e-12, scalar2=None, op0=ALU.max)
+        nc.scalar.activation(out=wn[:], in_=wn[:], func=ACT.Sqrt)
+        nc.vector.tensor_scalar(out=wn[:], in0=wn[:], scalar1=qq[:, 0:1], scalar2=None, op0=ALU.add)
+        rw = const.tile([P, 512], F32)
+        nc.vector.reciprocal(out=rw[:], in_=wn[:])
+        wg = epi.tile([P, 2, 512, 4], BF16, tag="big", align_bytes=64)
+        w4 = w_raw[:].rearrange("p (t g) n -> p t g n", g=2)
+        for g in range(2):
+            nc.vector.tensor_tensor(
+                out=wg[:, g, :, :],
+                in0=w4[:, :, g, :].rearrange("p t n -> p n t"),
+                in1=rw[:].unsqueeze(2).to_broadcast([P, 512, 4]),
+                op=ALU.mult,
+            )
+        wcodes = const.tile([P, 1024], U32, align_bytes=64)
+        wscl = const.tile([P, 1024], U8, align_bytes=64)
+        nc.vector.quantize_mx(
+            out=wcodes[:].bitcast(FP8X4),
+            scales=wscl[:],
+            in_=wg[:].rearrange("p g n t -> p (g n t)"),
+        )
+        pe = const.tile([P, 512], F32)
+        nc.scalar.activation(out=pe[:], in_=p_bc[:], func=ACT.Square, scale=0.2)
+
+        out_v = out.rearrange("b y z u -> (b y) z u")
+        st = {}
+
+        def scale_and_transpose(qd):
+            h, z0 = qd // 8, 4 * (qd % 8)
+            sc = work.tile([P, 4, 4, 256], BF16, tag="sc")
+            for zi in range(4):
+                for bq in range(4):
+                    b, z = 4 * h + bq, z0 + zi
+                    nc.vector.tensor_scalar(
+                        out=sc[:, zi, bq, :],
+                        in0=xs2[:, b, 64 * z : 64 * z + 256],
+                        scalar1=rn[:, 32 * b + z : 32 * b + z + 1],
+                        scalar2=None,
+                        op0=ALU.mult,
+                    )
+            xts = []
+            for zi in range(4):
+                xt = psum.tile([P, 2, 4, 128], BF16, tag="xt")
+                for g in range(2):
+                    for bq in range(4):
+                        nc.tensor.transpose(
+                            out=xt[:, g, bq, :],
+                            in_=sc[:, zi, bq, 128 * g : 128 * g + 128],
+                            identity=perm[:],
+                        )
+                xts.append(xt)
+            st[("xt", qd)] = xts
+
+        def exits(qd):
+            grp = work.tile([P, 4, 1024], BF16, tag="grp", align_bytes=64)
+            xts = st[("xt", qd)]
+            for zi in range(4):
+                src = xts[zi][:].rearrange("p g b n -> p (g b n)")
+                if zi in S_EXITS:
+                    nc.scalar.copy(out=grp[:, zi, :], in_=src)
+                else:
+                    nc.vector.tensor_copy(out=grp[:, zi, :], in_=src)
+            st[("grp", qd)] = grp
+
+        def quant_and_mx(qd):
+            grp = st[("grp", qd)]
+            codes = work.tile([P, 1024], U32, tag="codes", align_bytes=64)
+            scl = work.tile([P, 1024], U8, tag="scl", align_bytes=64)
+            nc.vector.quantize_mx(
+                out=codes[:].bitcast(FP8X4),
+                scales=scl[:],
+                in_=grp[:].rearrange("p z n -> p (z n)"),
+            )
+            accs = []
+            for zi in range(4):
+                acc = psum.tile([P, 512], F32, tag="acc")
+                for g in range(2):
+                    c0 = 256 * zi + 128 * g
+                    nc.tensor.matmul_mx(
+                        out=acc[:],
+                        lhsT=codes[:, c0 : c0 + 128].bitcast(FP8X4),
+                        lhsT_scale=scl[:, c0 : c0 + 128],
+                        rhs=wcodes[:, 512 * g : 512 * g + 512].bitcast(FP8X4),
+                        rhs_scale=wscl[:, 512 * g : 512 * g + 512],
+                        start=(g == 0),
+                        stop=(g == 1),
+                    )
+                accs.append(acc)
+            st[("acc", qd)] = accs
+
+        def sign_abs(qd):
+            accs = st[("acc", qd)]
+            sg = epi.tile([P, 4, 512], BF16, tag="sg")
+            av = epi.tile([P, 4, 512], F32, tag="big", align_bytes=64)
+            for zi in range(4):
+                nc.scalar.activation(out=sg[:, zi, :], in_=accs[zi][:], func=ACT.Sign)
+                nc.vector.tensor_tensor(out=av[:, zi, :], in0=accs[zi][:], in1=sg[:, zi, :], op=ALU.mult)
+            st[("sg", qd)] = sg
+            st[("av", qd)] = av
+
+        def ln(qd):
+            av = st[("av", qd)]
+            nc.scalar.activation(out=av[:], in_=av[:], func=ACT.Ln, bias=eps_t[:, 0:1])
+
+        def times_pe(qd):
+            av = st[("av", qd)]
+            nc.vector.tensor_tensor(
+                out=av[:], in0=av[:], in1=pe[:].unsqueeze(1).to_broadcast([P, 4, 512]), op=ALU.mult
+            )
+
+        def exp_apply_store(qd):
+            h, z0 = qd // 8, 4 * (qd % 8)
+            av = st[("av", qd)]
+            nc.scalar.activation(out=av[:], in_=av[:], func=ACT.Exp)
+            nc.gpsimd.tensor_tensor(out=av[:], in0=av[:], in1=st[("sg", qd)][:], op=ALU.mult)
+            nc.sync.dma_start(out=out_v[128 * h : 128 * h + 128, z0 : z0 + 4, :], in_=av[:])
+
+        tasks = []
+        for ch in CHUNKS:
+            tasks.extend([("L", qd) for qd in ch])
+            tasks.extend([("E", qd) for qd in ch])
+        have_abs, have_ln, have_pe = set(), [], set()
+        pos = [0, 0]
+
+        def run_task():
+            if pos[0] >= len(tasks):
+                return
+            kind, qd = tasks[pos[0]]
+            if kind == "L" and qd in have_abs:
+                ln(qd)
+                have_ln.append(qd)
+                pos[0] += 1
+            elif kind == "E" and qd in have_pe:
+                exp_apply_store(qd)
+                pos[0] += 1
+
+        def run_pe():
+            if pos[1] < len(have_ln):
+                qd = have_ln[pos[1]]
+                times_pe(qd)
+                have_pe.add(qd)
+                pos[1] += 1
+
+        if MANUAL:
+            ctx.enter_context(tc.manual_schedule())
+        for t in range(40):
+            if t < NQ:
+                scale_and_transpose(t)
+            if 1 <= t <= NQ:
+                quant_and_mx(t - 1)
+            run_task()
+            run_pe()
+            if t < NQ:
+                exits(t)
+            run_task()
+            if t > NQ:
+                run_pe()
+            if 1 <= t <= NQ:
+                sign_abs(t - 1)
+                have_abs.add(t - 1)
+        assert pos[0] == len(tasks)

@@ -18,8 +18,32 @@ P = 128
 ROW = 35 * 64
 NQ = 16
 MANUAL = True
-S_EXITS = (1, 3)
-CHUNKS = ((0, 1, 2, 3), (4, 5, 6, 7), (8, 9, 10, 11), (12, 13), (14, 15))
+PE_PSUM = True
+XT_BUFS = 3
+ACC_BUFS = 4
+EPI_BUFS = 8
+SPLIT = 15
+NORM2_S = 2
+S_EXIT = (1, 0, 1, 0)
+S_FIRST = 0
+CHUNKS = ((0, 1, 2, 3), (4, 5, 6, 7), (8, 9, 10, 11), (12, 13, 14, 15))
+PW = 1
+TASKS_A = 1
+TASKS_B = 1
+PES = 2
+APPLIES = 1
+APPLY_V = False
+TAIL_V = True
+LLAG = 3
+ELAG = 1
+GLAG = 1
+ILAG = 1
+DYN_EXIT = True
+S_LAST = 64
+PE_S = 5
+ROW_TILE_START = (0, 105, 152)
+IMG_TILE = (0, 0, 0, 1, 1, 1, 2, 2)
+OFFSETS = (0, 35, 70, 58, 93)
 
 
 def tile_cossim2d_t_kernel(tc, x, w, p, q, out):
@@ -27,33 +51,41 @@ def tile_cossim2d_t_kernel(tc, x, w, p, q, out):
     with ExitStack() as ctx:
         const = ctx.enter_context(tc.tile_pool(name="const", bufs=1))
         work = ctx.enter_context(tc.tile_pool(name="work", bufs=2))
-        epi = ctx.enter_context(tc.tile_pool(name="epi", bufs=8))
+        epi = ctx.enter_context(tc.tile_pool(name="epi", bufs=EPI_BUFS))
         psum = ctx.enter_context(tc.psum_pool(name="psum", bufs=4))
+        if MANUAL:
+            ctx.enter_context(tc.manual_schedule())
 
         x_rows = x.rearrange("b h w c -> (b h) (w c)")
         xr = []
         for k in range(3):
             xr_k = epi.tile([P, ROW], BF16, tag="sg", name="xr%d" % k)
             xr.append(xr_k)
-        nc.vector.memset(xr[2][:], 0.0)
-        nc.sync.dma_start(out=xr[0][:], in_=x_rows[0:128, :])
-        nc.sync.dma_start(out=xr[1][:], in_=x_rows[128:256, :])
-        nc.sync.dma_start(out=xr[2][0:24, :], in_=x_rows[256:280, :])
+        xs2 = const.tile([P, 8, ROW], BF16)
 
+        def load_rows(k):
+            r0 = ROW_TILE_START[k]
+            nc.sync.dma_start(out=xr[k][:], in_=x_rows[r0 : r0 + 128, :])
+
+        def load_shifted(h, c0, c1):
+            for i in (0, 2, 1, 3):
+                nc.sync.dma_start(
+                    out=xs2[32 * i : 32 * i + 32, 4 * h : 4 * h + 4, 64 * c0 : 64 * c1],
+                    in_=x[4 * h : 4 * h + 4, i : i + 32, c0:c1, :].rearrange("b y w c -> y b (w c)"),
+                )
+
+        load_rows(0)
+        load_rows(1)
         q_sb = const.tile([P, 1], BF16)
         nc.scalar.dma_start(out=q_sb[:], in_=q.partition_broadcast(P))
         w_raw = epi.tile([P, 8, 512], BF16, tag="big", align_bytes=64)
         nc.scalar.dma_start(out=w_raw[:], in_=w.rearrange("o (s p) n -> p (o s) n", p=P))
-        p_bc = const.tile([P, 512], BF16)
-        nc.scalar.dma_start(out=p_bc[:], in_=p.partition_broadcast(P))
-
-        xs2 = const.tile([P, 8, ROW], BF16)
-        for h in range(2):
-            for i in (0, 2, 1, 3):
-                nc.sync.dma_start(
-                    out=xs2[32 * i : 32 * i + 32, 4 * h : 4 * h + 4, :],
-                    in_=x[4 * h : 4 * h + 4, i : i + 32, :, :].rearrange("b y w c -> y b (w c)"),
-                )
+        p_row = const.tile([1, 512], BF16)
+        nc.scalar.dma_start(out=p_row[:], in_=p.unsqueeze(0))
+        load_shifted(0, 0, SPLIT)
+        load_rows(2)
+        load_shifted(0, SPLIT, 35)
+        load_shifted(1, 0, 35)
 
         eps_t = const.tile([P, 1], F32)
         nc.vector.memset(eps_t[:], 1e-6)
@@ -70,74 +102,108 @@ def tile_cossim2d_t_kernel(tc, x, w, p, q, out):
         )
         ones_f = const.tile([P, P], F32)
         nc.vector.memset(ones_f[:], 1.0)
-        iext = const.tile([P, 196], F32)
+        pe = const.tile([P, 512], F32)
+        nc.vector.memset(pe[:], 0.0)
+        iext = const.tile([P, 132], F32)
         nc.vector.memset(iext[:], 0.0)
-        nc.vector.tensor_copy(out=iext[:, 32:160], in_=ident_f[:])
-        band = const.tile([P, 192], F32)
-        nc.vector.tensor_tensor(out=band[:], in0=iext[:, 0:192], in1=iext[:, 1:193], op=ALU.add)
-        nc.vector.tensor_tensor(out=band[:], in0=band[:], in1=iext[:, 2:194], op=ALU.add)
-        nc.vector.tensor_tensor(out=band[:], in0=band[:], in1=iext[:, 3:195], op=ALU.add)
-        pairs = ((0, 0), (1, 0), (2, 0), (3, 0), (3, 1), (4, 1), (5, 1), (6, 1), (7, 1), (7, 2))
-        sel = const.tile([P, 10, 4, 32], F32)
-        for idx, (b, k) in enumerate(pairs):
-            o = 32 + 35 * b - 128 * k
+        nc.vector.tensor_copy(out=iext[:, 0:128], in_=ident_f[:])
+        band = const.tile([P, 128], F32)
+        nc.vector.tensor_tensor(out=band[:], in0=iext[:, 0:128], in1=iext[:, 1:129], op=ALU.add)
+        nc.vector.tensor_tensor(out=band[:], in0=band[:], in1=iext[:, 2:130], op=ALU.add)
+        nc.vector.tensor_tensor(out=band[:], in0=band[:], in1=iext[:, 3:131], op=ALU.add)
+        sel = const.tile([P, 5, 4, 32], F32)
+        for idx, o in enumerate(OFFSETS):
             nc.vector.tensor_copy(
                 out=sel[:, idx, :, :],
                 in_=band[:, o : o + 32].unsqueeze(1).to_broadcast([P, 4, 32]),
             )
-        qq = const.tile([P, 1], F32)
-        nc.scalar.activation(out=qq[:], in_=q_sb[:], func=ACT.Square, scale=1.0 / 0.3)
 
         csum = const.tile([P, 3, 35], F32)
-        for k in range(3):
+        rsum = const.tile([P, 3, 32], F32)
+        qq = const.tile([P, 1], F32)
+        xn = const.tile([P, 256], F32)
+        rn = const.tile([P, 256], F32)
+
+        def row_squares(k):
             sq = epi.tile([P, ROW], F32, tag="big", align_bytes=64)
             nc.scalar.activation(out=sq[:], in_=xr[k][:], func=ACT.Square)
-            nc.vector.tensor_reduce(
-                out=csum[:, k, :],
-                in_=sq[:].rearrange("p (w c) -> p w c", c=64),
-                axis=AX.X,
-                op=ALU.add,
-            )
-        rsum = const.tile([P, 3, 32], F32)
-        nc.vector.tensor_tensor(out=rsum[:], in0=csum[:, :, 0:32], in1=csum[:, :, 1:33], op=ALU.add)
-        nc.vector.tensor_tensor(out=rsum[:], in0=rsum[:], in1=csum[:, :, 2:34], op=ALU.add)
-        nc.vector.tensor_tensor(out=rsum[:], in0=rsum[:], in1=csum[:, :, 3:35], op=ALU.add)
-        ss = psum.tile([P, 256], F32, tag="acc")
-        for idx, (b, k) in enumerate(pairs):
-            first = idx == 0 or pairs[idx - 1][0] != b
-            last = idx == 9 or pairs[idx + 1][0] != b
-            nc.tensor.matmul(
-                out=ss[:, 32 * b : 32 * b + 32],
-                lhsT=sel[:, idx, :, :].rearrange("p i y -> p (i y)"),
-                rhs=rsum[:, k, :],
-                start=first,
-                stop=last,
-            )
-        xn = const.tile([P, 256], F32)
-        nc.vector.tensor_scalar(out=xn[:], in0=ss[:], scalar1=1e-12, scalar2=None, op0=ALU.max)
-        nc.scalar.activation(out=xn[:], in_=xn[:], func=ACT.Sqrt)
-        nc.vector.tensor_scalar(out=xn[:], in0=xn[:], scalar1=qq[:, 0:1], scalar2=None, op0=ALU.add)
-        rn = const.tile([P, 256], F32)
-        nc.vector.reciprocal(out=rn[:], in_=xn[:])
+            return sq
 
-        wss = psum.tile([P, 512], F32, tag="acc")
-        for hh in range(2):
-            wsq = epi.tile([P, 4, 512], F32, tag="big", align_bytes=64)
-            nc.scalar.activation(out=wsq[:], in_=w_raw[:, 4 * hh : 4 * hh + 4, :], func=ACT.Square)
-            for s in range(4):
+        def row_sums(k, sq):
+            nc.vector.tensor_reduce(
+                out=csum[:, k, :], in_=sq[:].rearrange("p (w c) -> p w c", c=64), axis=AX.X, op=ALU.add
+            )
+            nc.vector.tensor_tensor(out=rsum[:, k, :], in0=csum[:, k, 0:32], in1=csum[:, k, 1:33], op=ALU.add)
+            nc.vector.tensor_tensor(out=rsum[:, k, :], in0=rsum[:, k, :], in1=csum[:, k, 2:34], op=ALU.add)
+            nc.vector.tensor_tensor(out=rsum[:, k, :], in0=rsum[:, k, :], in1=csum[:, k, 3:35], op=ALU.add)
+
+        def patch_norms(h):
+            ss = psum.tile([P, 128], F32, tag="xt", bufs=XT_BUFS)
+            for bq in range(4):
+                b = 4 * h + bq
+                k = IMG_TILE[b]
+                idx = OFFSETS.index(35 * b - ROW_TILE_START[k])
                 nc.tensor.matmul(
-                    out=wss[:],
-                    lhsT=ones_f[:],
-                    rhs=wsq[:, s, :],
-                    start=(hh == 0 and s == 0),
-                    stop=(hh == 1 and s == 3),
+                    out=ss[:, 32 * bq : 32 * bq + 32],
+                    lhsT=sel[:, idx, :, :].rearrange("p i y -> p (i y)"),
+                    rhs=rsum[:, k, :],
+                    start=True,
+                    stop=True,
                 )
-        wn = const.tile([P, 512], F32)
-        nc.vector.tensor_scalar(out=wn[:], in0=wss[:], scalar1=1e-12, scalar2=None, op0=ALU.max)
-        nc.scalar.activation(out=wn[:], in_=wn[:], func=ACT.Sqrt)
-        nc.vector.tensor_scalar(out=wn[:], in0=wn[:], scalar1=qq[:, 0:1], scalar2=None, op0=ALU.add)
-        rw = const.tile([P, 512], F32)
-        nc.vector.reciprocal(out=rw[:], in_=wn[:])
+            half = slice(128 * h, 128 * h + 128)
+            nc.vector.tensor_scalar(out=xn[:, half], in0=ss[:], scalar1=1e-12, scalar2=None, op0=ALU.max)
+            nc.scalar.activation(out=xn[:, half], in_=xn[:, half], func=ACT.Sqrt)
+            nc.vector.tensor_scalar(out=xn[:, half], in0=xn[:, half], scalar1=qq[:, 0:1], scalar2=None, op0=ALU.add)
+            nc.vector.reciprocal(out=rn[:, half], in_=xn[:, half])
+
+        sq0 = row_squares(0)
+        nc.scalar.activation(out=qq[:], in_=q_sb[:], func=ACT.Square, scale=1.0 / 0.3)
+        sq1 = row_squares(1)
+        row_sums(0, sq0)
+        row_sums(1, sq1)
+
+        st = {}
+
+        def scale(qd):
+            h, z0 = qd // 8, 4 * (qd % 8)
+            sc = work.tile([P, 4, 4, 256], BF16, tag="sc")
+            for zi in range(4):
+                for bq in range(4):
+                    b, z = 4 * h + bq, z0 + zi
+                    nc.vector.tensor_scalar(
+                        out=sc[:, zi, bq, :],
+                        in0=xs2[:, b, 64 * z : 64 * z + 256],
+                        scalar1=rn[:, 32 * b + z : 32 * b + z + 1],
+                        scalar2=None,
+                        op0=ALU.mult,
+                    )
+            st[("sc", qd)] = sc
+
+        wss = const.tile([P, 4], F32)
+        for ub in range(4):
+            wt = psum.tile([P, 8, 128], BF16, tag="acc", bufs=ACC_BUFS)
+            for s in range(8):
+                nc.tensor.transpose(out=wt[:, s, :], in_=w_raw[:, s, 128 * ub : 128 * ub + 128], identity=ident_bf[:])
+            wjunk = epi.tile([P, 1024], BF16, tag="sg")
+            nc.scalar.activation(
+                out=wjunk[:], in_=wt[:].rearrange("p s k -> p (s k)"), func=ACT.Square, accum_out=wss[:, ub : ub + 1]
+            )
+        patch_norms(0)
+        nc.vector.tensor_scalar(out=wss[:], in0=wss[:], scalar1=1e-12, scalar2=None, op0=ALU.max)
+        nc.scalar.activation(out=wss[:], in_=wss[:], func=ACT.Sqrt)
+        nc.vector.tensor_scalar(out=wss[:], in0=wss[:], scalar1=qq[:, 0:1], scalar2=None, op0=ALU.add)
+        rwc = const.tile([P, 4], F32)
+        nc.vector.reciprocal(out=rwc[:], in_=wss[:])
+        rw = psum.tile([P, 512], F32, tag="acc", bufs=ACC_BUFS)
+        for ub in range(4):
+            nc.tensor.matmul(
+                out=rw[:, 128 * ub : 128 * ub + 128],
+                lhsT=rwc[:, ub : ub + 1].to_broadcast([P, P]),
+                rhs=ident_f[:],
+                start=True,
+                stop=True,
+            )
+        scale(0)
         wg = epi.tile([P, 2, 512, 4], BF16, tag="big", align_bytes=64)
         w4 = w_raw[:].rearrange("p (t g) n -> p t g n", g=2)
         for g in range(2):
@@ -154,143 +220,184 @@ def tile_cossim2d_t_kernel(tc, x, w, p, q, out):
             scales=wscl[:],
             in_=wg[:].rearrange("p g n t -> p (g n t)"),
         )
-        pe = const.tile([P, 512], F32)
-        nc.scalar.activation(out=pe[:], in_=p_bc[:], func=ACT.Square, scale=0.2)
 
+        pe_ps = psum.tile([P, 512], F32, tag="pe", bufs=1)
+        pe_op = pe_ps
         out_v = out.rearrange("b y z u -> (b y) z u")
-        st = {}
+        NG = 64
 
-        def scale_and_transpose(qd):
-            h, z0 = qd // 8, 4 * (qd % 8)
-            sc = work.tile([P, 4, 4, 256], BF16, tag="sc")
-            for zi in range(4):
+        def transposes(n):
+            qd, zi = n // 4, n % 4
+            sc = st[("sc", qd)]
+            xt = psum.tile([P, 2, 4, 128], BF16, tag="xt", bufs=XT_BUFS)
+            for g in range(2):
                 for bq in range(4):
-                    b, z = 4 * h + bq, z0 + zi
-                    nc.vector.tensor_scalar(
-                        out=sc[:, zi, bq, :],
-                        in0=xs2[:, b, 64 * z : 64 * z + 256],
-                        scalar1=rn[:, 32 * b + z : 32 * b + z + 1],
-                        scalar2=None,
-                        op0=ALU.mult,
+                    nc.tensor.transpose(
+                        out=xt[:, g, bq, :], in_=sc[:, zi, bq, 128 * g : 128 * g + 128], identity=perm[:]
                     )
-            xts = []
-            for zi in range(4):
-                xt = psum.tile([P, 2, 4, 128], BF16, tag="xt")
-                for g in range(2):
-                    for bq in range(4):
-                        nc.tensor.transpose(
-                            out=xt[:, g, bq, :],
-                            in_=sc[:, zi, bq, 128 * g : 128 * g + 128],
-                            identity=perm[:],
-                        )
-                xts.append(xt)
-            st[("xt", qd)] = xts
+            st[("xt", n)] = xt
 
-        def exits(qd):
-            grp = work.tile([P, 4, 1024], BF16, tag="grp", align_bytes=64)
-            xts = st[("xt", qd)]
-            for zi in range(4):
-                src = xts[zi][:].rearrange("p g b n -> p (g b n)")
-                if zi in S_EXITS:
-                    nc.scalar.copy(out=grp[:, zi, :], in_=src)
-                else:
-                    nc.vector.tensor_copy(out=grp[:, zi, :], in_=src)
-            st[("grp", qd)] = grp
+        def leave(n):
+            qd, zi = n // 4, n % 4
+            if zi == 0:
+                grp_new = work.tile([P, 4, 1024], BF16, tag="grp", align_bytes=64)
+                st[("grp", qd)] = grp_new
+            grp = st[("grp", qd)]
+            src = st[("xt", n)][:].rearrange("p g b n -> p (g b n)")
+            on_s = S_EXIT[n % len(S_EXIT)]
+            if DYN_EXIT:
+                on_s = pos[0] >= len(tasks) or tasks[pos[0]][0] == "L"
+            if n < S_FIRST or (on_s and n < S_LAST):
+                nc.scalar.copy(out=grp[:, zi, :], in_=src)
+            else:
+                nc.vector.tensor_copy(out=grp[:, zi, :], in_=src)
 
-        def quant_and_mx(qd):
+        def quant(qd):
             grp = st[("grp", qd)]
             codes = work.tile([P, 1024], U32, tag="codes", align_bytes=64)
             scl = work.tile([P, 1024], U8, tag="scl", align_bytes=64)
             nc.vector.quantize_mx(
-                out=codes[:].bitcast(FP8X4),
-                scales=scl[:],
-                in_=grp[:].rearrange("p z n -> p (z n)"),
+                out=codes[:].bitcast(FP8X4), scales=scl[:], in_=grp[:].rearrange("p z n -> p (z n)")
             )
-            accs = []
-            for zi in range(4):
-                acc = psum.tile([P, 512], F32, tag="acc")
-                for g in range(2):
-                    c0 = 256 * zi + 128 * g
-                    nc.tensor.matmul_mx(
-                        out=acc[:],
-                        lhsT=codes[:, c0 : c0 + 128].bitcast(FP8X4),
-                        lhsT_scale=scl[:, c0 : c0 + 128],
-                        rhs=wcodes[:, 512 * g : 512 * g + 512].bitcast(FP8X4),
-                        rhs_scale=wscl[:, 512 * g : 512 * g + 512],
-                        start=(g == 0),
-                        stop=(g == 1),
-                    )
-                accs.append(acc)
-            st[("acc", qd)] = accs
+            st[("codes", qd)] = (codes, scl)
 
-        def sign_abs(qd):
-            accs = st[("acc", qd)]
-            sg = epi.tile([P, 4, 512], BF16, tag="sg")
-            av = epi.tile([P, 4, 512], F32, tag="big", align_bytes=64)
-            for zi in range(4):
-                nc.scalar.activation(out=sg[:, zi, :], in_=accs[zi][:], func=ACT.Sign)
-                nc.vector.tensor_tensor(out=av[:, zi, :], in0=accs[zi][:], in1=sg[:, zi, :], op=ALU.mult)
-            st[("sg", qd)] = sg
-            st[("av", qd)] = av
+        def mx(n):
+            qd, zi = n // 4, n % 4
+            codes, scl = st[("codes", qd)]
+            acc = psum.tile([P, 512], F32, tag="acc", bufs=ACC_BUFS)
+            for g in range(2):
+                c0 = 256 * zi + 128 * g
+                nc.tensor.matmul_mx(
+                    out=acc[:],
+                    lhsT=codes[:, c0 : c0 + 128].bitcast(FP8X4),
+                    lhsT_scale=scl[:, c0 : c0 + 128],
+                    rhs=wcodes[:, 512 * g : 512 * g + 512].bitcast(FP8X4),
+                    rhs_scale=wscl[:, 512 * g : 512 * g + 512],
+                    start=(g == 0),
+                    stop=(g == 1),
+                )
+            st[("acc", n)] = acc
 
-        def ln(qd):
-            av = st[("av", qd)]
-            nc.scalar.activation(out=av[:], in_=av[:], func=ACT.Ln, bias=eps_t[:, 0:1])
+        def sign(n):
+            qd, zi = n // 4, n % 4
+            if zi == 0:
+                sg_new = epi.tile([P, 4, 512], BF16, tag="sg")
+                av_new = epi.tile([P, 4, 512], F32, tag="big", align_bytes=64)
+                st[("sg", qd)] = sg_new
+                st[("av", qd)] = av_new
+            nc.scalar.activation(out=st[("sg", qd)][:, zi, :], in_=st[("acc", n)][:], func=ACT.Sign)
 
-        def times_pe(qd):
-            av = st[("av", qd)]
+        def absval(n):
+            qd, zi = n // 4, n % 4
             nc.vector.tensor_tensor(
-                out=av[:], in0=av[:], in1=pe[:].unsqueeze(1).to_broadcast([P, 4, 512]), op=ALU.mult
+                out=st[("av", qd)][:, zi, :], in0=st[("acc", n)][:], in1=st[("sg", qd)][:, zi, :], op=ALU.mult
             )
 
-        def exp_apply_store(qd):
+        def piece(qd, lo, hi):
+            return st[("av", qd)][:, lo:hi, :]
+
+        def ln(qd, lo, hi):
+            nc.scalar.activation(out=piece(qd, lo, hi), in_=piece(qd, lo, hi), func=ACT.Ln, bias=eps_t[:, 0:1])
+
+        def times_pe(qd, lo, hi):
+            nc.vector.tensor_tensor(
+                out=piece(qd, lo, hi),
+                in0=piece(qd, lo, hi),
+                in1=pe_op[:].unsqueeze(1).to_broadcast([P, hi - lo, 512]),
+                op=ALU.mult,
+            )
+
+        def expo(qd, lo, hi):
+            nc.scalar.activation(out=piece(qd, lo, hi), in_=piece(qd, lo, hi), func=ACT.Exp)
+
+        def apply_sign(qd, lo, hi, eng):
+            eng.tensor_tensor(
+                out=piece(qd, lo, hi), in0=piece(qd, lo, hi), in1=st[("sg", qd)][:, lo:hi, :], op=ALU.mult
+            )
+
+        def store(qd):
             h, z0 = qd // 8, 4 * (qd % 8)
-            av = st[("av", qd)]
-            nc.scalar.activation(out=av[:], in_=av[:], func=ACT.Exp)
-            nc.gpsimd.tensor_tensor(out=av[:], in0=av[:], in1=st[("sg", qd)][:], op=ALU.mult)
-            nc.sync.dma_start(out=out_v[128 * h : 128 * h + 128, z0 : z0 + 4, :], in_=av[:])
+            nc.sync.dma_start(out=out_v[128 * h : 128 * h + 128, z0 : z0 + 4, :], in_=st[("av", qd)][:])
 
         tasks = []
         for ch in CHUNKS:
-            tasks.extend([("L", qd) for qd in ch])
-            tasks.extend([("E", qd) for qd in ch])
-        have_abs, have_ln, have_pe = set(), [], set()
-        pos = [0, 0]
+            for kind in ("L", "E"):
+                for qd in ch:
+                    for lo in range(0, 4, PW):
+                        tasks.append((kind, qd, lo))
+        have_abs, have_ln, have_pe, have_exp = set(), [], {}, []
+        pos = [0, 0, 0]
+        now = [0]
 
         def run_task():
             if pos[0] >= len(tasks):
                 return
-            kind, qd = tasks[pos[0]]
-            if kind == "L" and qd in have_abs:
-                ln(qd)
-                have_ln.append(qd)
+            kind, qd, lo = tasks[pos[0]]
+            if kind == "L" and 4 * qd + lo + PW - 1 <= now[0] - 3 - LLAG:
+                ln(qd, lo, lo + PW)
+                have_ln.append((qd, lo, now[0]))
                 pos[0] += 1
-            elif kind == "E" and qd in have_pe:
-                exp_apply_store(qd)
+            elif kind == "E" and have_pe.get((qd, lo), 999) <= now[0] - ELAG:
+                expo(qd, lo, lo + PW)
+                have_exp.append((qd, lo, now[0]))
                 pos[0] += 1
 
         def run_pe():
-            if pos[1] < len(have_ln):
-                qd = have_ln[pos[1]]
-                times_pe(qd)
-                have_pe.add(qd)
+            if pos[1] < len(have_ln) and have_ln[pos[1]][2] <= now[0] - GLAG:
+                qd, lo, when = have_ln[pos[1]]
+                times_pe(qd, lo, lo + PW)
+                have_pe[(qd, lo)] = now[0]
                 pos[1] += 1
 
-        if MANUAL:
-            ctx.enter_context(tc.manual_schedule())
-        for t in range(40):
-            if t < NQ:
-                scale_and_transpose(t)
-            if 1 <= t <= NQ:
-                quant_and_mx(t - 1)
-            run_task()
-            run_pe()
-            if t < NQ:
-                exits(t)
-            run_task()
-            if t > NQ:
+        def run_apply(last):
+            if pos[2] < len(have_exp) and have_exp[pos[2]][2] <= now[0] - ILAG:
+                qd, lo, when = have_exp[pos[2]]
+                eng = nc.vector if (APPLY_V or (last and TAIL_V)) else nc.gpsimd
+                apply_sign(qd, lo, lo + PW, eng)
+                if lo + PW == 4:
+                    store(qd)
+                pos[2] += 1
+
+        scale(1)
+        for s in range(-4, 64 + 200):
+            if pos[0] >= len(tasks) and pos[2] >= len(have_exp):
+                break
+            tail = s > NG + 3
+            now[0] = s
+            if s == PE_S:
+                nc.scalar.activation(out=pe[0:1, :], in_=p_row[:], func=ACT.Square, scale=0.2)
+            if s == PE_S + 1:
+                nc.tensor.matmul(out=pe_ps[:], lhsT=ones_f[:], rhs=pe[:], start=True, stop=True)
+            if s == NORM2_S:
+                st["sq2"] = row_squares(2)
+            if s == NORM2_S + 1:
+                row_sums(2, st["sq2"])
+            if s == NORM2_S + 2:
+                patch_norms(1)
+            if s % 4 == 1 and 0 <= s // 4 < NQ:
+                quant(s // 4)
+                if s // 4 + 2 < NQ:
+                    scale(s // 4 + 2)
+            if 0 <= s - 2 < NG:
+                mx(s - 2)
+            if 0 <= s + 4 < NG:
+                transposes(s + 4)
+            for r in range(TASKS_A):
+                run_task()
+            if 0 <= s - 3 < NG:
+                sign(s - 3)
+                absval(s - 3)
+                have_abs.add(s - 3)
+            if 0 <= s + 3 < NG:
+                leave(s + 3)
+            for r in range(TASKS_B):
+                run_task()
+            for r in range(PES if not tail else 4):
                 run_pe()
-            if 1 <= t <= NQ:
-                sign_abs(t - 1)
-                have_abs.add(t - 1)
-        assert pos[0] == len(tasks)
+            for r in range(APPLIES if not tail else 4):
+                run_apply(tail)
+            if tail:
+                run_task()
+                run_pe()
+                run_apply(tail)
+        assert pos[0] == len(tasks) and pos[2] == len(have_exp)

@@ -17,7 +17,7 @@ FLOPS = 2 * 8192 * 1024 * 512
 P = 128
 ROW = 35 * 64
 NQ = 16
-MANUAL = True
+MANUAL = False
 PE_PSUM = True
 XT_BUFS = 3
 ACC_BUFS = 4
@@ -41,6 +41,10 @@ ILAG = 1
 DYN_EXIT = True
 S_LAST = 64
 PE_S = 5
+G_PE = 0
+G_PE_LAST = 64
+S_SCALE = ()
+FINE_STORE = 16
 ROW_TILE_START = (0, 105, 152)
 IMG_TILE = (0, 0, 0, 1, 1, 1, 2, 2)
 OFFSETS = (0, 35, 70, 58, 93)
@@ -137,7 +141,7 @@ def tile_cossim2d_t_kernel(tc, x, w, p, q, out):
             nc.vector.tensor_tensor(out=rsum[:, k, :], in0=rsum[:, k, :], in1=csum[:, k, 2:34], op=ALU.add)
             nc.vector.tensor_tensor(out=rsum[:, k, :], in0=rsum[:, k, :], in1=csum[:, k, 3:35], op=ALU.add)
 
-        def patch_norms(h):
+        def patch_sums(h):
             ss = psum.tile([P, 128], F32, tag="xt", bufs=XT_BUFS)
             for bq in range(4):
                 b = 4 * h + bq
@@ -150,6 +154,9 @@ def tile_cossim2d_t_kernel(tc, x, w, p, q, out):
                     start=True,
                     stop=True,
                 )
+            return ss
+
+        def patch_norms(h, ss):
             half = slice(128 * h, 128 * h + 128)
             nc.vector.tensor_scalar(out=xn[:, half], in0=ss[:], scalar1=1e-12, scalar2=None, op0=ALU.max)
             nc.scalar.activation(out=xn[:, half], in_=xn[:, half], func=ACT.Sqrt)
@@ -167,9 +174,18 @@ def tile_cossim2d_t_kernel(tc, x, w, p, q, out):
         def scale(qd):
             h, z0 = qd // 8, 4 * (qd % 8)
             sc = work.tile([P, 4, 4, 256], BF16, tag="sc")
+            st[("sc", qd)] = sc
             for zi in range(4):
                 for bq in range(4):
                     b, z = 4 * h + bq, z0 + zi
+                    if qd in S_SCALE:
+                        nc.scalar.activation(
+                            out=sc[:, zi, bq, :],
+                            in_=xs2[:, b, 64 * z : 64 * z + 256],
+                            func=ACT.Copy,
+                            scale=rn[:, 32 * b + z : 32 * b + z + 1],
+                        )
+                        continue
                     nc.vector.tensor_scalar(
                         out=sc[:, zi, bq, :],
                         in0=xs2[:, b, 64 * z : 64 * z + 256],
@@ -188,12 +204,13 @@ def tile_cossim2d_t_kernel(tc, x, w, p, q, out):
             nc.scalar.activation(
                 out=wjunk[:], in_=wt[:].rearrange("p s k -> p (s k)"), func=ACT.Square, accum_out=wss[:, ub : ub + 1]
             )
-        patch_norms(0)
+        ss0 = patch_sums(0)
         nc.vector.tensor_scalar(out=wss[:], in0=wss[:], scalar1=1e-12, scalar2=None, op0=ALU.max)
         nc.scalar.activation(out=wss[:], in_=wss[:], func=ACT.Sqrt)
         nc.vector.tensor_scalar(out=wss[:], in0=wss[:], scalar1=qq[:, 0:1], scalar2=None, op0=ALU.add)
         rwc = const.tile([P, 4], F32)
         nc.vector.reciprocal(out=rwc[:], in_=wss[:])
+        patch_norms(0, ss0)
         rw = psum.tile([P, 512], F32, tag="acc", bufs=ACC_BUFS)
         for ub in range(4):
             nc.tensor.matmul(
@@ -223,6 +240,7 @@ def tile_cossim2d_t_kernel(tc, x, w, p, q, out):
 
         pe_ps = psum.tile([P, 512], F32, tag="pe", bufs=1)
         pe_op = pe_ps
+        pe_sb = const.tile([P, 512], F32)
         out_v = out.rearrange("b y z u -> (b y) z u")
         NG = 64
 
@@ -299,13 +317,21 @@ def tile_cossim2d_t_kernel(tc, x, w, p, q, out):
         def ln(qd, lo, hi):
             nc.scalar.activation(out=piece(qd, lo, hi), in_=piece(qd, lo, hi), func=ACT.Ln, bias=eps_t[:, 0:1])
 
-        def times_pe(qd, lo, hi):
-            nc.vector.tensor_tensor(
-                out=piece(qd, lo, hi),
-                in0=piece(qd, lo, hi),
-                in1=pe_op[:].unsqueeze(1).to_broadcast([P, hi - lo, 512]),
-                op=ALU.mult,
-            )
+        def times_pe(qd, lo, hi, on_g):
+            if on_g:
+                nc.gpsimd.tensor_tensor(
+                    out=piece(qd, lo, hi),
+                    in0=piece(qd, lo, hi),
+                    in1=pe_sb[:].unsqueeze(1).to_broadcast([P, hi - lo, 512]),
+                    op=ALU.mult,
+                )
+            else:
+                nc.vector.tensor_tensor(
+                    out=piece(qd, lo, hi),
+                    in0=piece(qd, lo, hi),
+                    in1=pe_op[:].unsqueeze(1).to_broadcast([P, hi - lo, 512]),
+                    op=ALU.mult,
+                )
 
         def expo(qd, lo, hi):
             nc.scalar.activation(out=piece(qd, lo, hi), in_=piece(qd, lo, hi), func=ACT.Exp)
@@ -345,7 +371,7 @@ def tile_cossim2d_t_kernel(tc, x, w, p, q, out):
         def run_pe():
             if pos[1] < len(have_ln) and have_ln[pos[1]][2] <= now[0] - GLAG:
                 qd, lo, when = have_ln[pos[1]]
-                times_pe(qd, lo, lo + PW)
+                times_pe(qd, lo, lo + PW, G_PE > 0 and pos[1] % G_PE == G_PE - 1 and pos[1] < G_PE_LAST)
                 have_pe[(qd, lo)] = now[0]
                 pos[1] += 1
 
@@ -354,7 +380,12 @@ def tile_cossim2d_t_kernel(tc, x, w, p, q, out):
                 qd, lo, when = have_exp[pos[2]]
                 eng = nc.vector if (APPLY_V or (last and TAIL_V)) else nc.gpsimd
                 apply_sign(qd, lo, lo + PW, eng)
-                if lo + PW == 4:
+                if qd >= FINE_STORE:
+                    h, z0 = qd // 8, 4 * (qd % 8)
+                    nc.sync.dma_start(
+                        out=out_v[128 * h : 128 * h + 128, z0 + lo : z0 + lo + PW, :], in_=piece(qd, lo, lo + PW)
+                    )
+                elif lo + PW == 4:
                     store(qd)
                 pos[2] += 1
 
@@ -368,12 +399,14 @@ def tile_cossim2d_t_kernel(tc, x, w, p, q, out):
                 nc.scalar.activation(out=pe[0:1, :], in_=p_row[:], func=ACT.Square, scale=0.2)
             if s == PE_S + 1:
                 nc.tensor.matmul(out=pe_ps[:], lhsT=ones_f[:], rhs=pe[:], start=True, stop=True)
+            if s == PE_S + 2 and G_PE > 0:
+                nc.vector.tensor_copy(out=pe_sb[:], in_=pe_ps[:])
             if s == NORM2_S:
                 st["sq2"] = row_squares(2)
             if s == NORM2_S + 1:
                 row_sums(2, st["sq2"])
             if s == NORM2_S + 2:
-                patch_norms(1)
+                patch_norms(1, patch_sums(1))
             if s % 4 == 1 and 0 <= s // 4 < NQ:
                 quant(s // 4)
                 if s // 4 + 2 < NQ:

@@ -17,12 +17,12 @@ FLOPS = 2 * 8192 * 1024 * 512
 P = 128
 ROW = 35 * 64
 NQ = 16
-MANUAL = False
+MANUAL = True
 PE_PSUM = True
 XT_BUFS = 3
 ACC_BUFS = 4
 EPI_BUFS = 8
-SPLIT = 15
+SPLIT = 11
 NORM2_S = 2
 S_EXIT = (1, 0, 1, 0)
 S_FIRST = 0
@@ -44,7 +44,10 @@ PE_S = 5
 G_PE = 0
 G_PE_LAST = 64
 S_SCALE = ()
-FINE_STORE = 16
+FINE_STORE = 12
+G_PE_KEEP = 4
+DYN_MOD = 99
+TWO_QUEUES = True
 ROW_TILE_START = (0, 105, 152)
 IMG_TILE = (0, 0, 0, 1, 1, 1, 2, 2)
 OFFSETS = (0, 35, 70, 58, 93)
@@ -73,7 +76,8 @@ def tile_cossim2d_t_kernel(tc, x, w, p, q, out):
 
         def load_shifted(h, c0, c1):
             for i in (0, 2, 1, 3):
-                nc.sync.dma_start(
+                queue = nc.scalar if (TWO_QUEUES and i >= 2) else nc.sync
+                queue.dma_start(
                     out=xs2[32 * i : 32 * i + 32, 4 * h : 4 * h + 4, 64 * c0 : 64 * c1],
                     in_=x[4 * h : 4 * h + 4, i : i + 32, c0:c1, :].rearrange("b y w c -> y b (w c)"),
                 )
@@ -264,7 +268,7 @@ def tile_cossim2d_t_kernel(tc, x, w, p, q, out):
             src = st[("xt", n)][:].rearrange("p g b n -> p (g b n)")
             on_s = S_EXIT[n % len(S_EXIT)]
             if DYN_EXIT:
-                on_s = pos[0] >= len(tasks) or tasks[pos[0]][0] == "L"
+                on_s = pos[0] >= len(tasks) or (tasks[pos[0]][0] == "L" and n % DYN_MOD != DYN_MOD - 1)
             if n < S_FIRST or (on_s and n < S_LAST):
                 nc.scalar.copy(out=grp[:, zi, :], in_=src)
             else:
@@ -368,10 +372,19 @@ def tile_cossim2d_t_kernel(tc, x, w, p, q, out):
                 have_exp.append((qd, lo, now[0]))
                 pos[0] += 1
 
+        def on_gpsimd(qd, lo):
+            if G_PE == 0:
+                return False
+            for ch in CHUNKS:
+                if qd in ch:
+                    j = 4 * ch.index(qd) + lo
+                    return j % G_PE == G_PE - 1 and j < 4 * len(ch) - G_PE_KEEP
+            return False
+
         def run_pe():
             if pos[1] < len(have_ln) and have_ln[pos[1]][2] <= now[0] - GLAG:
                 qd, lo, when = have_ln[pos[1]]
-                times_pe(qd, lo, lo + PW, G_PE > 0 and pos[1] % G_PE == G_PE - 1 and pos[1] < G_PE_LAST)
+                times_pe(qd, lo, lo + PW, on_gpsimd(qd, lo))
                 have_pe[(qd, lo)] = now[0]
                 pos[1] += 1
 

@@ -16,41 +16,16 @@ FLOPS = 2 * 8192 * 1024 * 512
 
 P = 128
 ROW = 35 * 64
-NQ = 16
-MANUAL = True
-PE_PSUM = True
-XT_BUFS = 3
-ACC_BUFS = 4
-EPI_BUFS = 8
-SPLIT = 11
-NORM2_S = 2
-S_EXIT = (1, 0, 1, 0)
-S_FIRST = 0
-CHUNKS = ((0, 1, 2, 3), (4, 5, 6, 7), (8, 9, 10, 11), (12, 13, 14, 15))
-PW = 1
-TASKS_A = 1
-TASKS_B = 1
-PES = 2
-APPLIES = 1
-APPLY_V = False
-TAIL_V = True
-LLAG = 3
-ELAG = 1
-GLAG = 1
-ILAG = 1
-DYN_EXIT = True
-S_LAST = 64
-PE_S = 5
-G_PE = 0
-G_PE_LAST = 64
-S_SCALE = ()
-FINE_STORE = 12
-G_PE_KEEP = 4
-DYN_MOD = 99
-TWO_QUEUES = True
+GROUPS = 64
+QUADS = 16
 ROW_TILE_START = (0, 105, 152)
-IMG_TILE = (0, 0, 0, 1, 1, 1, 2, 2)
-OFFSETS = (0, 35, 70, 58, 93)
+ROW_TILE_OF = (0, 0, 0, 1, 1, 1, 2, 2)
+IMAGE_STARTS = (0, 35, 70, 58, 93)
+FIRST_PIXELS = 11
+CHUNKS = ((0, 1, 2, 3), (4, 5, 6, 7), (8, 9, 10, 11), (12, 13, 14, 15))
+FIRST_FINE_STORE = 12
+LN_LAG = 3
+NEXT_LAG = 1
 
 
 def tile_cossim2d_t_kernel(tc, x, w, p, q, out):
@@ -58,47 +33,45 @@ def tile_cossim2d_t_kernel(tc, x, w, p, q, out):
     with ExitStack() as ctx:
         const = ctx.enter_context(tc.tile_pool(name="const", bufs=1))
         work = ctx.enter_context(tc.tile_pool(name="work", bufs=2))
-        epi = ctx.enter_context(tc.tile_pool(name="epi", bufs=EPI_BUFS))
+        epi = ctx.enter_context(tc.tile_pool(name="epi", bufs=8))
         psum = ctx.enter_context(tc.psum_pool(name="psum", bufs=4))
-        if MANUAL:
-            ctx.enter_context(tc.manual_schedule())
+        ctx.enter_context(tc.manual_schedule())
 
         x_rows = x.rearrange("b h w c -> (b h) (w c)")
-        xr = []
+        rows = []
         for k in range(3):
-            xr_k = epi.tile([P, ROW], BF16, tag="sg", name="xr%d" % k)
-            xr.append(xr_k)
-        xs2 = const.tile([P, 8, ROW], BF16)
+            rows_k = epi.tile([P, ROW], BF16, tag="sign", name="rows%d" % k)
+            rows.append(rows_k)
+        shifted = const.tile([P, 8, ROW], BF16)
 
         def load_rows(k):
             r0 = ROW_TILE_START[k]
-            nc.sync.dma_start(out=xr[k][:], in_=x_rows[r0 : r0 + 128, :])
+            nc.sync.dma_start(out=rows[k][:], in_=x_rows[r0 : r0 + 128, :])
 
-        def load_shifted(h, c0, c1):
+        def load_shifted(half, c0, c1):
             for i in (0, 2, 1, 3):
-                queue = nc.scalar if (TWO_QUEUES and i >= 2) else nc.sync
-                queue.dma_start(
-                    out=xs2[32 * i : 32 * i + 32, 4 * h : 4 * h + 4, 64 * c0 : 64 * c1],
-                    in_=x[4 * h : 4 * h + 4, i : i + 32, c0:c1, :].rearrange("b y w c -> y b (w c)"),
+                nc.sync.dma_start(
+                    out=shifted[32 * i : 32 * i + 32, 4 * half : 4 * half + 4, 64 * c0 : 64 * c1],
+                    in_=x[4 * half : 4 * half + 4, i : i + 32, c0:c1, :].rearrange("b y w c -> y b (w c)"),
                 )
 
         load_rows(0)
         load_rows(1)
         q_sb = const.tile([P, 1], BF16)
         nc.scalar.dma_start(out=q_sb[:], in_=q.partition_broadcast(P))
-        w_raw = epi.tile([P, 8, 512], BF16, tag="big", align_bytes=64)
-        nc.scalar.dma_start(out=w_raw[:], in_=w.rearrange("o (s p) n -> p (o s) n", p=P))
+        w_raw = epi.tile([P, 8, 512], BF16, tag="value", align_bytes=64)
+        nc.scalar.dma_start(out=w_raw[:], in_=w.rearrange("o (s r) n -> r (o s) n", r=P))
         p_row = const.tile([1, 512], BF16)
         nc.scalar.dma_start(out=p_row[:], in_=p.unsqueeze(0))
-        load_shifted(0, 0, SPLIT)
+        load_shifted(0, 0, FIRST_PIXELS)
         load_rows(2)
-        load_shifted(0, SPLIT, 35)
+        load_shifted(0, FIRST_PIXELS, 35)
         load_shifted(1, 0, 35)
 
         eps_t = const.tile([P, 1], F32)
         nc.vector.memset(eps_t[:], 1e-6)
-        junk = const.tile([P, 1], F32)
-        nc.scalar.activation(out=junk[:], in_=eps_t[:], func=ACT.Sqrt)
+        warm = const.tile([P, 1], F32)
+        nc.scalar.activation(out=warm[:], in_=eps_t[:], func=ACT.Sqrt)
         ident_bf = const.tile([P, P], BF16)
         make_identity(nc, ident_bf[:])
         ident_f = const.tile([P, P], F32)
@@ -110,62 +83,70 @@ def tile_cossim2d_t_kernel(tc, x, w, p, q, out):
         )
         ones_f = const.tile([P, P], F32)
         nc.vector.memset(ones_f[:], 1.0)
-        pe = const.tile([P, 512], F32)
-        nc.vector.memset(pe[:], 0.0)
-        iext = const.tile([P, 132], F32)
-        nc.vector.memset(iext[:], 0.0)
-        nc.vector.tensor_copy(out=iext[:, 0:128], in_=ident_f[:])
+        expo_row = const.tile([P, 512], F32)
+        nc.vector.memset(expo_row[:], 0.0)
+        ident_wide = const.tile([P, 132], F32)
+        nc.vector.memset(ident_wide[:], 0.0)
+        nc.vector.tensor_copy(out=ident_wide[:, 0:128], in_=ident_f[:])
         band = const.tile([P, 128], F32)
-        nc.vector.tensor_tensor(out=band[:], in0=iext[:, 0:128], in1=iext[:, 1:129], op=ALU.add)
-        nc.vector.tensor_tensor(out=band[:], in0=band[:], in1=iext[:, 2:130], op=ALU.add)
-        nc.vector.tensor_tensor(out=band[:], in0=band[:], in1=iext[:, 3:131], op=ALU.add)
-        sel = const.tile([P, 5, 4, 32], F32)
-        for idx, o in enumerate(OFFSETS):
+        nc.vector.tensor_tensor(out=band[:], in0=ident_wide[:, 0:128], in1=ident_wide[:, 1:129], op=ALU.add)
+        nc.vector.tensor_tensor(out=band[:], in0=band[:], in1=ident_wide[:, 2:130], op=ALU.add)
+        nc.vector.tensor_tensor(out=band[:], in0=band[:], in1=ident_wide[:, 3:131], op=ALU.add)
+        gather = const.tile([P, 5, 4, 32], F32)
+        for n, start in enumerate(IMAGE_STARTS):
             nc.vector.tensor_copy(
-                out=sel[:, idx, :, :],
-                in_=band[:, o : o + 32].unsqueeze(1).to_broadcast([P, 4, 32]),
+                out=gather[:, n, :, :],
+                in_=band[:, start : start + 32].unsqueeze(1).to_broadcast([P, 4, 32]),
             )
 
-        csum = const.tile([P, 3, 35], F32)
-        rsum = const.tile([P, 3, 32], F32)
+        pixel_sq = const.tile([P, 3, 35], F32)
+        window_sq = const.tile([P, 3, 32], F32)
         qq = const.tile([P, 1], F32)
-        xn = const.tile([P, 256], F32)
-        rn = const.tile([P, 256], F32)
+        x_norm = const.tile([P, 256], F32)
+        x_scale = const.tile([P, 256], F32)
 
         def row_squares(k):
-            sq = epi.tile([P, ROW], F32, tag="big", align_bytes=64)
-            nc.scalar.activation(out=sq[:], in_=xr[k][:], func=ACT.Square)
+            sq = epi.tile([P, ROW], F32, tag="value", align_bytes=64)
+            nc.scalar.activation(out=sq[:], in_=rows[k][:], func=ACT.Square)
             return sq
 
         def row_sums(k, sq):
             nc.vector.tensor_reduce(
-                out=csum[:, k, :], in_=sq[:].rearrange("p (w c) -> p w c", c=64), axis=AX.X, op=ALU.add
+                out=pixel_sq[:, k, :], in_=sq[:].rearrange("p (w c) -> p w c", c=64), axis=AX.X, op=ALU.add
             )
-            nc.vector.tensor_tensor(out=rsum[:, k, :], in0=csum[:, k, 0:32], in1=csum[:, k, 1:33], op=ALU.add)
-            nc.vector.tensor_tensor(out=rsum[:, k, :], in0=rsum[:, k, :], in1=csum[:, k, 2:34], op=ALU.add)
-            nc.vector.tensor_tensor(out=rsum[:, k, :], in0=rsum[:, k, :], in1=csum[:, k, 3:35], op=ALU.add)
+            nc.vector.tensor_tensor(
+                out=window_sq[:, k, :], in0=pixel_sq[:, k, 0:32], in1=pixel_sq[:, k, 1:33], op=ALU.add
+            )
+            nc.vector.tensor_tensor(
+                out=window_sq[:, k, :], in0=window_sq[:, k, :], in1=pixel_sq[:, k, 2:34], op=ALU.add
+            )
+            nc.vector.tensor_tensor(
+                out=window_sq[:, k, :], in0=window_sq[:, k, :], in1=pixel_sq[:, k, 3:35], op=ALU.add
+            )
 
-        def patch_sums(h):
-            ss = psum.tile([P, 128], F32, tag="xt", bufs=XT_BUFS)
+        def patch_sums(half):
+            sums = psum.tile([P, 128], F32, tag="turned", bufs=3)
             for bq in range(4):
-                b = 4 * h + bq
-                k = IMG_TILE[b]
-                idx = OFFSETS.index(35 * b - ROW_TILE_START[k])
+                b = 4 * half + bq
+                k = ROW_TILE_OF[b]
+                n = IMAGE_STARTS.index(35 * b - ROW_TILE_START[k])
                 nc.tensor.matmul(
-                    out=ss[:, 32 * bq : 32 * bq + 32],
-                    lhsT=sel[:, idx, :, :].rearrange("p i y -> p (i y)"),
-                    rhs=rsum[:, k, :],
+                    out=sums[:, 32 * bq : 32 * bq + 32],
+                    lhsT=gather[:, n, :, :].rearrange("p i y -> p (i y)"),
+                    rhs=window_sq[:, k, :],
                     start=True,
                     stop=True,
                 )
-            return ss
+            return sums
 
-        def patch_norms(h, ss):
-            half = slice(128 * h, 128 * h + 128)
-            nc.vector.tensor_scalar(out=xn[:, half], in0=ss[:], scalar1=1e-12, scalar2=None, op0=ALU.max)
-            nc.scalar.activation(out=xn[:, half], in_=xn[:, half], func=ACT.Sqrt)
-            nc.vector.tensor_scalar(out=xn[:, half], in0=xn[:, half], scalar1=qq[:, 0:1], scalar2=None, op0=ALU.add)
-            nc.vector.reciprocal(out=rn[:, half], in_=xn[:, half])
+        def patch_norms(half, sums):
+            cols = slice(128 * half, 128 * half + 128)
+            nc.vector.tensor_scalar(out=x_norm[:, cols], in0=sums[:], scalar1=1e-12, scalar2=None, op0=ALU.max)
+            nc.scalar.activation(out=x_norm[:, cols], in_=x_norm[:, cols], func=ACT.Sqrt)
+            nc.vector.tensor_scalar(
+                out=x_norm[:, cols], in0=x_norm[:, cols], scalar1=qq[:, 0:1], scalar2=None, op0=ALU.add
+            )
+            nc.vector.reciprocal(out=x_scale[:, cols], in_=x_norm[:, cols])
 
         sq0 = row_squares(0)
         nc.scalar.activation(out=qq[:], in_=q_sb[:], func=ACT.Square, scale=1.0 / 0.3)
@@ -173,277 +154,222 @@ def tile_cossim2d_t_kernel(tc, x, w, p, q, out):
         row_sums(0, sq0)
         row_sums(1, sq1)
 
-        st = {}
+        live = {}
 
-        def scale(qd):
-            h, z0 = qd // 8, 4 * (qd % 8)
-            sc = work.tile([P, 4, 4, 256], BF16, tag="sc")
-            st[("sc", qd)] = sc
+        def scale(quad):
+            half, z0 = quad // 8, 4 * (quad % 8)
+            scaled = work.tile([P, 4, 4, 256], BF16, tag="scaled")
+            live[("scaled", quad)] = scaled
             for zi in range(4):
                 for bq in range(4):
-                    b, z = 4 * h + bq, z0 + zi
-                    if qd in S_SCALE:
-                        nc.scalar.activation(
-                            out=sc[:, zi, bq, :],
-                            in_=xs2[:, b, 64 * z : 64 * z + 256],
-                            func=ACT.Copy,
-                            scale=rn[:, 32 * b + z : 32 * b + z + 1],
-                        )
-                        continue
+                    b, z = 4 * half + bq, z0 + zi
                     nc.vector.tensor_scalar(
-                        out=sc[:, zi, bq, :],
-                        in0=xs2[:, b, 64 * z : 64 * z + 256],
-                        scalar1=rn[:, 32 * b + z : 32 * b + z + 1],
+                        out=scaled[:, zi, bq, :],
+                        in0=shifted[:, b, 64 * z : 64 * z + 256],
+                        scalar1=x_scale[:, 32 * b + z : 32 * b + z + 1],
                         scalar2=None,
                         op0=ALU.mult,
                     )
-            st[("sc", qd)] = sc
 
-        wss = const.tile([P, 4], F32)
+        w_norm = const.tile([P, 4], F32)
         for ub in range(4):
-            wt = psum.tile([P, 8, 128], BF16, tag="acc", bufs=ACC_BUFS)
+            w_turned = psum.tile([P, 8, 128], BF16, tag="acc", bufs=4)
             for s in range(8):
-                nc.tensor.transpose(out=wt[:, s, :], in_=w_raw[:, s, 128 * ub : 128 * ub + 128], identity=ident_bf[:])
-            wjunk = epi.tile([P, 1024], BF16, tag="sg")
+                nc.tensor.transpose(
+                    out=w_turned[:, s, :], in_=w_raw[:, s, 128 * ub : 128 * ub + 128], identity=ident_bf[:]
+                )
+            unused = epi.tile([P, 1024], BF16, tag="sign")
             nc.scalar.activation(
-                out=wjunk[:], in_=wt[:].rearrange("p s k -> p (s k)"), func=ACT.Square, accum_out=wss[:, ub : ub + 1]
+                out=unused[:],
+                in_=w_turned[:].rearrange("p s k -> p (s k)"),
+                func=ACT.Square,
+                accum_out=w_norm[:, ub : ub + 1],
             )
-        ss0 = patch_sums(0)
-        nc.vector.tensor_scalar(out=wss[:], in0=wss[:], scalar1=1e-12, scalar2=None, op0=ALU.max)
-        nc.scalar.activation(out=wss[:], in_=wss[:], func=ACT.Sqrt)
-        nc.vector.tensor_scalar(out=wss[:], in0=wss[:], scalar1=qq[:, 0:1], scalar2=None, op0=ALU.add)
-        rwc = const.tile([P, 4], F32)
-        nc.vector.reciprocal(out=rwc[:], in_=wss[:])
-        patch_norms(0, ss0)
-        rw = psum.tile([P, 512], F32, tag="acc", bufs=ACC_BUFS)
+        sums0 = patch_sums(0)
+        nc.vector.tensor_scalar(out=w_norm[:], in0=w_norm[:], scalar1=1e-12, scalar2=None, op0=ALU.max)
+        nc.scalar.activation(out=w_norm[:], in_=w_norm[:], func=ACT.Sqrt)
+        nc.vector.tensor_scalar(out=w_norm[:], in0=w_norm[:], scalar1=qq[:, 0:1], scalar2=None, op0=ALU.add)
+        w_scale_col = const.tile([P, 4], F32)
+        nc.vector.reciprocal(out=w_scale_col[:], in_=w_norm[:])
+        patch_norms(0, sums0)
+        w_scale = psum.tile([P, 512], F32, tag="acc", bufs=4)
         for ub in range(4):
             nc.tensor.matmul(
-                out=rw[:, 128 * ub : 128 * ub + 128],
-                lhsT=rwc[:, ub : ub + 1].to_broadcast([P, P]),
+                out=w_scale[:, 128 * ub : 128 * ub + 128],
+                lhsT=w_scale_col[:, ub : ub + 1].to_broadcast([P, P]),
                 rhs=ident_f[:],
                 start=True,
                 stop=True,
             )
         scale(0)
-        wg = epi.tile([P, 2, 512, 4], BF16, tag="big", align_bytes=64)
-        w4 = w_raw[:].rearrange("p (t g) n -> p t g n", g=2)
+        w_grouped = epi.tile([P, 2, 512, 4], BF16, tag="value", align_bytes=64)
+        w_tg = w_raw[:].rearrange("p (t g) n -> p t g n", g=2)
         for g in range(2):
             nc.vector.tensor_tensor(
-                out=wg[:, g, :, :],
-                in0=w4[:, :, g, :].rearrange("p t n -> p n t"),
-                in1=rw[:].unsqueeze(2).to_broadcast([P, 512, 4]),
+                out=w_grouped[:, g, :, :],
+                in0=w_tg[:, :, g, :].rearrange("p t n -> p n t"),
+                in1=w_scale[:].unsqueeze(2).to_broadcast([P, 512, 4]),
                 op=ALU.mult,
             )
-        wcodes = const.tile([P, 1024], U32, align_bytes=64)
-        wscl = const.tile([P, 1024], U8, align_bytes=64)
+        w_codes = const.tile([P, 1024], U32, align_bytes=64)
+        w_scales = const.tile([P, 1024], U8, align_bytes=64)
         nc.vector.quantize_mx(
-            out=wcodes[:].bitcast(FP8X4),
-            scales=wscl[:],
-            in_=wg[:].rearrange("p g n t -> p (g n t)"),
+            out=w_codes[:].bitcast(FP8X4),
+            scales=w_scales[:],
+            in_=w_grouped[:].rearrange("p g n t -> p (g n t)"),
         )
 
-        pe_ps = psum.tile([P, 512], F32, tag="pe", bufs=1)
-        pe_op = pe_ps
-        pe_sb = const.tile([P, 512], F32)
+        expo = psum.tile([P, 512], F32, tag="expo", bufs=1)
         out_v = out.rearrange("b y z u -> (b y) z u")
-        NG = 64
 
         def transposes(n):
-            qd, zi = n // 4, n % 4
-            sc = st[("sc", qd)]
-            xt = psum.tile([P, 2, 4, 128], BF16, tag="xt", bufs=XT_BUFS)
+            quad, zi = n // 4, n % 4
+            scaled = live[("scaled", quad)]
+            turned = psum.tile([P, 2, 4, 128], BF16, tag="turned", bufs=3)
             for g in range(2):
                 for bq in range(4):
                     nc.tensor.transpose(
-                        out=xt[:, g, bq, :], in_=sc[:, zi, bq, 128 * g : 128 * g + 128], identity=perm[:]
+                        out=turned[:, g, bq, :], in_=scaled[:, zi, bq, 128 * g : 128 * g + 128], identity=perm[:]
                     )
-            st[("xt", n)] = xt
+            live[("turned", n)] = turned
 
-        def leave(n):
-            qd, zi = n // 4, n % 4
+        def leave_psum(n, engine_is_scalar):
+            quad, zi = n // 4, n % 4
             if zi == 0:
-                grp_new = work.tile([P, 4, 1024], BF16, tag="grp", align_bytes=64)
-                st[("grp", qd)] = grp_new
-            grp = st[("grp", qd)]
-            src = st[("xt", n)][:].rearrange("p g b n -> p (g b n)")
-            on_s = S_EXIT[n % len(S_EXIT)]
-            if DYN_EXIT:
-                on_s = pos[0] >= len(tasks) or (tasks[pos[0]][0] == "L" and n % DYN_MOD != DYN_MOD - 1)
-            if n < S_FIRST or (on_s and n < S_LAST):
-                nc.scalar.copy(out=grp[:, zi, :], in_=src)
+                grouped_new = work.tile([P, 4, 1024], BF16, tag="grouped", align_bytes=64)
+                live[("grouped", quad)] = grouped_new
+            grouped = live[("grouped", quad)]
+            turned = live[("turned", n)][:].rearrange("p g b n -> p (g b n)")
+            if engine_is_scalar:
+                nc.scalar.copy(out=grouped[:, zi, :], in_=turned)
             else:
-                nc.vector.tensor_copy(out=grp[:, zi, :], in_=src)
+                nc.vector.tensor_copy(out=grouped[:, zi, :], in_=turned)
 
-        def quant(qd):
-            grp = st[("grp", qd)]
+        def quantise(quad):
             codes = work.tile([P, 1024], U32, tag="codes", align_bytes=64)
-            scl = work.tile([P, 1024], U8, tag="scl", align_bytes=64)
+            scales = work.tile([P, 1024], U8, tag="scales", align_bytes=64)
             nc.vector.quantize_mx(
-                out=codes[:].bitcast(FP8X4), scales=scl[:], in_=grp[:].rearrange("p z n -> p (z n)")
+                out=codes[:].bitcast(FP8X4),
+                scales=scales[:],
+                in_=live[("grouped", quad)][:].rearrange("p z n -> p (z n)"),
             )
-            st[("codes", qd)] = (codes, scl)
+            live[("codes", quad)] = (codes, scales)
 
-        def mx(n):
-            qd, zi = n // 4, n % 4
-            codes, scl = st[("codes", qd)]
-            acc = psum.tile([P, 512], F32, tag="acc", bufs=ACC_BUFS)
+        def multiply(n):
+            quad, zi = n // 4, n % 4
+            codes, scales = live[("codes", quad)]
+            acc = psum.tile([P, 512], F32, tag="acc", bufs=4)
             for g in range(2):
                 c0 = 256 * zi + 128 * g
                 nc.tensor.matmul_mx(
                     out=acc[:],
                     lhsT=codes[:, c0 : c0 + 128].bitcast(FP8X4),
-                    lhsT_scale=scl[:, c0 : c0 + 128],
-                    rhs=wcodes[:, 512 * g : 512 * g + 512].bitcast(FP8X4),
-                    rhs_scale=wscl[:, 512 * g : 512 * g + 512],
+                    lhsT_scale=scales[:, c0 : c0 + 128],
+                    rhs=w_codes[:, 512 * g : 512 * g + 512].bitcast(FP8X4),
+                    rhs_scale=w_scales[:, 512 * g : 512 * g + 512],
                     start=(g == 0),
                     stop=(g == 1),
                 )
-            st[("acc", n)] = acc
+            live[("acc", n)] = acc
 
-        def sign(n):
-            qd, zi = n // 4, n % 4
+        def sign_and_abs(n):
+            quad, zi = n // 4, n % 4
             if zi == 0:
-                sg_new = epi.tile([P, 4, 512], BF16, tag="sg")
-                av_new = epi.tile([P, 4, 512], F32, tag="big", align_bytes=64)
-                st[("sg", qd)] = sg_new
-                st[("av", qd)] = av_new
-            nc.scalar.activation(out=st[("sg", qd)][:, zi, :], in_=st[("acc", n)][:], func=ACT.Sign)
+                sign_new = epi.tile([P, 4, 512], BF16, tag="sign")
+                value_new = epi.tile([P, 4, 512], F32, tag="value", align_bytes=64)
+                live[("sign", quad)] = sign_new
+                live[("value", quad)] = value_new
+            acc = live[("acc", n)]
+            sign = live[("sign", quad)][:, zi, :]
+            nc.scalar.activation(out=sign, in_=acc[:], func=ACT.Sign)
+            nc.vector.tensor_tensor(out=live[("value", quad)][:, zi, :], in0=acc[:], in1=sign, op=ALU.mult)
 
-        def absval(n):
-            qd, zi = n // 4, n % 4
-            nc.vector.tensor_tensor(
-                out=st[("av", qd)][:, zi, :], in0=st[("acc", n)][:], in1=st[("sg", qd)][:, zi, :], op=ALU.mult
+        def value(n):
+            return live[("value", n // 4)][:, n % 4, :]
+
+        def store(n, count):
+            half, z = n // 32, n % 32
+            nc.sync.dma_start(
+                out=out_v[128 * half : 128 * half + 128, z : z + count, :],
+                in_=live[("value", n // 4)][:, n % 4 : n % 4 + count, :],
             )
 
-        def piece(qd, lo, hi):
-            return st[("av", qd)][:, lo:hi, :]
+        long_work = []
+        for chunk in CHUNKS:
+            for func in (ACT.Ln, ACT.Exp):
+                long_work.extend([(func, 4 * quad + zi) for quad in chunk for zi in range(4)])
+        done = [0, 0, 0]
+        logs, powers = [], []
+        multiplied = {}
 
-        def ln(qd, lo, hi):
-            nc.scalar.activation(out=piece(qd, lo, hi), in_=piece(qd, lo, hi), func=ACT.Ln, bias=eps_t[:, 0:1])
+        def next_is_ln():
+            return done[0] >= len(long_work) or long_work[done[0]][0] == ACT.Ln
 
-        def times_pe(qd, lo, hi, on_g):
-            if on_g:
-                nc.gpsimd.tensor_tensor(
-                    out=piece(qd, lo, hi),
-                    in0=piece(qd, lo, hi),
-                    in1=pe_sb[:].unsqueeze(1).to_broadcast([P, hi - lo, 512]),
-                    op=ALU.mult,
-                )
-            else:
-                nc.vector.tensor_tensor(
-                    out=piece(qd, lo, hi),
-                    in0=piece(qd, lo, hi),
-                    in1=pe_op[:].unsqueeze(1).to_broadcast([P, hi - lo, 512]),
-                    op=ALU.mult,
-                )
-
-        def expo(qd, lo, hi):
-            nc.scalar.activation(out=piece(qd, lo, hi), in_=piece(qd, lo, hi), func=ACT.Exp)
-
-        def apply_sign(qd, lo, hi, eng):
-            eng.tensor_tensor(
-                out=piece(qd, lo, hi), in0=piece(qd, lo, hi), in1=st[("sg", qd)][:, lo:hi, :], op=ALU.mult
-            )
-
-        def store(qd):
-            h, z0 = qd // 8, 4 * (qd % 8)
-            nc.sync.dma_start(out=out_v[128 * h : 128 * h + 128, z0 : z0 + 4, :], in_=st[("av", qd)][:])
-
-        tasks = []
-        for ch in CHUNKS:
-            for kind in ("L", "E"):
-                for qd in ch:
-                    for lo in range(0, 4, PW):
-                        tasks.append((kind, qd, lo))
-        have_abs, have_ln, have_pe, have_exp = set(), [], {}, []
-        pos = [0, 0, 0]
-        now = [0]
-
-        def run_task():
-            if pos[0] >= len(tasks):
+        def long_piece(step):
+            if done[0] >= len(long_work):
                 return
-            kind, qd, lo = tasks[pos[0]]
-            if kind == "L" and 4 * qd + lo + PW - 1 <= now[0] - 3 - LLAG:
-                ln(qd, lo, lo + PW)
-                have_ln.append((qd, lo, now[0]))
-                pos[0] += 1
-            elif kind == "E" and have_pe.get((qd, lo), 999) <= now[0] - ELAG:
-                expo(qd, lo, lo + PW)
-                have_exp.append((qd, lo, now[0]))
-                pos[0] += 1
+            func, n = long_work[done[0]]
+            if func == ACT.Ln and n + 3 + LN_LAG <= step:
+                nc.scalar.activation(out=value(n), in_=value(n), func=ACT.Ln, bias=eps_t[:, 0:1])
+                logs.append((n, step))
+                done[0] += 1
+            elif func == ACT.Exp and multiplied.get(n, step) + NEXT_LAG <= step:
+                nc.scalar.activation(out=value(n), in_=value(n), func=ACT.Exp)
+                powers.append((n, step))
+                done[0] += 1
 
-        def on_gpsimd(qd, lo):
-            if G_PE == 0:
-                return False
-            for ch in CHUNKS:
-                if qd in ch:
-                    j = 4 * ch.index(qd) + lo
-                    return j % G_PE == G_PE - 1 and j < 4 * len(ch) - G_PE_KEEP
-            return False
+        def times_exponent(step):
+            if done[1] < len(logs) and logs[done[1]][1] + NEXT_LAG <= step:
+                n = logs[done[1]][0]
+                nc.vector.tensor_tensor(out=value(n), in0=value(n), in1=expo[:], op=ALU.mult)
+                multiplied[n] = step
+                done[1] += 1
 
-        def run_pe():
-            if pos[1] < len(have_ln) and have_ln[pos[1]][2] <= now[0] - GLAG:
-                qd, lo, when = have_ln[pos[1]]
-                times_pe(qd, lo, lo + PW, on_gpsimd(qd, lo))
-                have_pe[(qd, lo)] = now[0]
-                pos[1] += 1
-
-        def run_apply(last):
-            if pos[2] < len(have_exp) and have_exp[pos[2]][2] <= now[0] - ILAG:
-                qd, lo, when = have_exp[pos[2]]
-                eng = nc.vector if (APPLY_V or (last and TAIL_V)) else nc.gpsimd
-                apply_sign(qd, lo, lo + PW, eng)
-                if qd >= FINE_STORE:
-                    h, z0 = qd // 8, 4 * (qd % 8)
-                    nc.sync.dma_start(
-                        out=out_v[128 * h : 128 * h + 128, z0 + lo : z0 + lo + PW, :], in_=piece(qd, lo, lo + PW)
-                    )
-                elif lo + PW == 4:
-                    store(qd)
-                pos[2] += 1
+        def times_sign(step, engine):
+            if done[2] < len(powers) and powers[done[2]][1] + NEXT_LAG <= step:
+                n = powers[done[2]][0]
+                engine.tensor_tensor(out=value(n), in0=value(n), in1=live[("sign", n // 4)][:, n % 4, :], op=ALU.mult)
+                if n // 4 >= FIRST_FINE_STORE:
+                    store(n, 1)
+                elif n % 4 == 3:
+                    store(n - 3, 4)
+                done[2] += 1
 
         scale(1)
-        for s in range(-4, 64 + 200):
-            if pos[0] >= len(tasks) and pos[2] >= len(have_exp):
+        for step in range(-4, 4 * GROUPS):
+            if done[0] >= len(long_work) and done[2] >= len(powers):
                 break
-            tail = s > NG + 3
-            now[0] = s
-            if s == PE_S:
-                nc.scalar.activation(out=pe[0:1, :], in_=p_row[:], func=ACT.Square, scale=0.2)
-            if s == PE_S + 1:
-                nc.tensor.matmul(out=pe_ps[:], lhsT=ones_f[:], rhs=pe[:], start=True, stop=True)
-            if s == PE_S + 2 and G_PE > 0:
-                nc.vector.tensor_copy(out=pe_sb[:], in_=pe_ps[:])
-            if s == NORM2_S:
-                st["sq2"] = row_squares(2)
-            if s == NORM2_S + 1:
-                row_sums(2, st["sq2"])
-            if s == NORM2_S + 2:
+            drained = step > GROUPS + 3
+            if step == 5:
+                nc.scalar.activation(out=expo_row[0:1, :], in_=p_row[:], func=ACT.Square, scale=0.2)
+            if step == 6:
+                nc.tensor.matmul(out=expo[:], lhsT=ones_f[:], rhs=expo_row[:], start=True, stop=True)
+            if step == 2:
+                live["sq2"] = row_squares(2)
+            if step == 3:
+                row_sums(2, live["sq2"])
+            if step == 4:
                 patch_norms(1, patch_sums(1))
-            if s % 4 == 1 and 0 <= s // 4 < NQ:
-                quant(s // 4)
-                if s // 4 + 2 < NQ:
-                    scale(s // 4 + 2)
-            if 0 <= s - 2 < NG:
-                mx(s - 2)
-            if 0 <= s + 4 < NG:
-                transposes(s + 4)
-            for r in range(TASKS_A):
-                run_task()
-            if 0 <= s - 3 < NG:
-                sign(s - 3)
-                absval(s - 3)
-                have_abs.add(s - 3)
-            if 0 <= s + 3 < NG:
-                leave(s + 3)
-            for r in range(TASKS_B):
-                run_task()
-            for r in range(PES if not tail else 4):
-                run_pe()
-            for r in range(APPLIES if not tail else 4):
-                run_apply(tail)
-            if tail:
-                run_task()
-                run_pe()
-                run_apply(tail)
-        assert pos[0] == len(tasks) and pos[2] == len(have_exp)
+            if step % 4 == 1 and 0 <= step // 4 < QUADS:
+                quantise(step // 4)
+                if step // 4 + 2 < QUADS:
+                    scale(step // 4 + 2)
+            if 0 <= step - 2 < GROUPS:
+                multiply(step - 2)
+            if 0 <= step + 4 < GROUPS:
+                transposes(step + 4)
+            long_piece(step)
+            if 0 <= step - 3 < GROUPS:
+                sign_and_abs(step - 3)
+            if 0 <= step + 3 < GROUPS:
+                leave_psum(step + 3, next_is_ln())
+            long_piece(step)
+            for repeat in range(4 if drained else 2):
+                times_exponent(step)
+            for repeat in range(4 if drained else 1):
+                times_sign(step, nc.vector if drained else nc.gpsimd)
+            if drained:
+                long_piece(step)
+                times_exponent(step)
+                times_sign(step, nc.vector)
+        assert done[0] == len(long_work) and done[2] == len(powers)

@@ -19,13 +19,16 @@ ROW = 35 * 64
 GROUPS = 64
 QUADS = 16
 ROW_TILE_START = (0, 105, 152)
-ROW_TILE_OF = (0, 0, 0, 1, 1, 1, 2, 2)
-IMAGE_STARTS = (0, 35, 70, 58, 93)
-FIRST_PIXELS = 11
-CHUNKS = ((0, 1, 2, 3), (4, 5, 6, 7), (8, 9, 10, 11), (12, 13, 14, 15))
-FIRST_FINE_STORE = 12
-LN_LAG = 3
-NEXT_LAG = 1
+IMAGE_AT = ((0, 0, 0, 0), (0, 1, 0, 35), (0, 2, 0, 70), (0, 3, 1, 0), (1, 0, 1, 35), (1, 1, 1, 70), (1, 2, 2, 58), (1, 3, 2, 93))
+ROW_TILES_OF = ((0, 1), (1, 2))
+FIRST_PIXELS = 19
+FIRST_Z = FIRST_PIXELS - 3
+CHUNKS = (32, 32)
+LEAD = 7
+SCALAR_COPIES = ((1, 1, 1, 0), (0, 0, 0, 0), (0, 1, 0, 1), (0, 0, 0, 0))
+GPSIMD_EXPO = ((0, 1, 0, 1), (0, 0, 0, 0), (0, 0, 0, 0), (0, 0, 0, 0))
+NORM_JOBS = ((0, 2, 19, 27, -2), (0, 2, 27, 35, -1), (2, 3, 0, 18, 0), (2, 3, 18, 35, 1))
+NORM_END = 3
 
 
 def tile_cossim2d_t_kernel(tc, x, w, p, q, out):
@@ -33,54 +36,55 @@ def tile_cossim2d_t_kernel(tc, x, w, p, q, out):
     with ExitStack() as ctx:
         const = ctx.enter_context(tc.tile_pool(name="const", bufs=1))
         work = ctx.enter_context(tc.tile_pool(name="work", bufs=2))
-        epi = ctx.enter_context(tc.tile_pool(name="epi", bufs=8))
+        epi = ctx.enter_context(tc.tile_pool(name="epi", bufs=20))
         psum = ctx.enter_context(tc.psum_pool(name="psum", bufs=4))
         ctx.enter_context(tc.manual_schedule())
 
         x_rows = x.rearrange("b h w c -> (b h) (w c)")
-        rows = []
-        for k in range(3):
-            rows_k = epi.tile([P, ROW], BF16, tag="sign", name="rows%d" % k)
-            rows.append(rows_k)
-        shifted = const.tile([P, 8, ROW], BF16)
+        rows = const.tile([P, 3, ROW], BF16)
+        shifted = const.tile([P, 2, 4, ROW], BF16)
 
-        def load_rows(k):
+        def load_rows(k, c0, c1):
             r0 = ROW_TILE_START[k]
-            nc.sync.dma_start(out=rows[k][:], in_=x_rows[r0 : r0 + 128, :])
+            nc.sync.dma_start(out=rows[:, k, 64 * c0 : 64 * c1], in_=x_rows[r0 : r0 + 128, 64 * c0 : 64 * c1])
 
         def load_shifted(half, c0, c1):
-            for i in (0, 2, 1, 3):
-                nc.sync.dma_start(
-                    out=shifted[32 * i : 32 * i + 32, 4 * half : 4 * half + 4, 64 * c0 : 64 * c1],
-                    in_=x[4 * half : 4 * half + 4, i : i + 32, c0:c1, :].rearrange("b y w c -> y b (w c)"),
-                )
+            for i in range(4):
+                for bq in (0, 2, 1, 3):
+                    nc.sync.dma_start(
+                        out=shifted[32 * bq : 32 * bq + 32, half, i, 64 * c0 : 64 * c1],
+                        in_=x[4 * half + bq, i : i + 32, c0:c1, :].rearrange("y w c -> y (w c)"),
+                    )
 
-        load_rows(0)
-        load_rows(1)
         q_sb = const.tile([P, 1], BF16)
         nc.scalar.dma_start(out=q_sb[:], in_=q.partition_broadcast(P))
-        w_raw = epi.tile([P, 8, 512], BF16, tag="value", align_bytes=64)
-        nc.scalar.dma_start(out=w_raw[:], in_=w.rearrange("o (s r) n -> r (o s) n", r=P))
         p_row = const.tile([1, 512], BF16)
         nc.scalar.dma_start(out=p_row[:], in_=p.unsqueeze(0))
+        load_rows(0, 0, FIRST_PIXELS)
+        load_rows(1, 0, FIRST_PIXELS)
+        w_rows = w.rearrange("o (s r) n -> r (o s) n", r=P)
+        w_raw = []
+        for h in range(2):
+            w_raw_h = epi.tile([P, 4, 512], BF16, tag="value", name="w_raw%d" % h)
+            nc.sync.dma_start(out=w_raw_h[:], in_=w_rows[:, 4 * h : 4 * h + 4, :])
+            w_raw.append(w_raw_h)
         load_shifted(0, 0, FIRST_PIXELS)
-        load_rows(2)
+        load_rows(0, FIRST_PIXELS, 35)
+        load_rows(1, FIRST_PIXELS, 35)
         load_shifted(0, FIRST_PIXELS, 35)
+        load_rows(2, 0, 35)
         load_shifted(1, 0, 35)
 
         eps_t = const.tile([P, 1], F32)
-        nc.vector.memset(eps_t[:], 1e-6)
+        nc.vector.memset(eps_t[:], 1.0)
         warm = const.tile([P, 1], F32)
         nc.scalar.activation(out=warm[:], in_=eps_t[:], func=ACT.Sqrt)
-        ident_bf = const.tile([P, P], BF16)
-        make_identity(nc, ident_bf[:])
+        nc.vector.memset(eps_t[:], 0.0)
+        nc.vector.tensor_scalar(out=eps_t[:], in0=eps_t[:], scalar1=1e-6, scalar2=None, op0=ALU.add)
         ident_f = const.tile([P, P], F32)
         make_identity(nc, ident_f[:])
-        perm = const.tile([P, P], BF16)
-        nc.vector.tensor_copy(
-            out=perm[:].rearrange("p (y i) -> p y i", i=4),
-            in_=ident_bf[:].rearrange("p (i y) -> p y i", i=4),
-        )
+        ident_bf = const.tile([P, P], BF16)
+        nc.vector.tensor_copy(out=ident_bf[:], in_=ident_f[:])
         ones_f = const.tile([P, P], F32)
         nc.vector.memset(ones_f[:], 1.0)
         expo_row = const.tile([P, 512], F32)
@@ -88,179 +92,258 @@ def tile_cossim2d_t_kernel(tc, x, w, p, q, out):
         ident_wide = const.tile([P, 132], F32)
         nc.vector.memset(ident_wide[:], 0.0)
         nc.vector.tensor_copy(out=ident_wide[:, 0:128], in_=ident_f[:])
+        pairs = const.tile([P, 130], F32)
+        nc.vector.tensor_tensor(out=pairs[:], in0=ident_wide[:, 0:130], in1=ident_wide[:, 1:131], op=ALU.add)
         band = const.tile([P, 128], F32)
-        nc.vector.tensor_tensor(out=band[:], in0=ident_wide[:, 0:128], in1=ident_wide[:, 1:129], op=ALU.add)
-        nc.vector.tensor_tensor(out=band[:], in0=band[:], in1=ident_wide[:, 2:130], op=ALU.add)
-        nc.vector.tensor_tensor(out=band[:], in0=band[:], in1=ident_wide[:, 3:131], op=ALU.add)
-        gather = const.tile([P, 5, 4, 32], F32)
-        for n, start in enumerate(IMAGE_STARTS):
+        nc.vector.tensor_tensor(out=band[:], in0=pairs[:, 0:128], in1=pairs[:, 2:130], op=ALU.add)
+        gather = const.tile([P, 2, 2, 128], F32)
+        nc.vector.memset(gather[:], 0.0)
+        for half, bq, k, start in IMAGE_AT:
             nc.vector.tensor_copy(
-                out=gather[:, n, :, :],
-                in_=band[:, start : start + 32].unsqueeze(1).to_broadcast([P, 4, 32]),
+                out=gather[:, half, ROW_TILES_OF[half].index(k), 32 * bq : 32 * bq + 32],
+                in_=band[:, start : start + 32],
             )
 
+        squares = const.tile([P, 2, 64 * FIRST_PIXELS], F32)
         pixel_sq = const.tile([P, 3, 35], F32)
+        two_sq = const.tile([P, 3, 34], F32)
         window_sq = const.tile([P, 3, 32], F32)
         qq = const.tile([P, 1], F32)
-        x_norm = const.tile([P, 256], F32)
-        x_scale = const.tile([P, 256], F32)
+        x_norm = const.tile([P, 64], F32)
+        x_scale = const.tile([P, 64], F32)
+        nc.scalar.activation(out=qq[:], in_=q_sb[:], func=ACT.Square, scale=1.0 / 0.3)
 
-        def row_squares(k):
-            sq = epi.tile([P, ROW], F32, tag="value", align_bytes=64)
-            nc.scalar.activation(out=sq[:], in_=rows[k][:], func=ACT.Square)
-            return sq
+        def squares_of(k0, k1, c0, c1, buf):
+            n = (k1 - k0) * (c1 - c0) * 64
+            base = buf * 64 * FIRST_PIXELS
+            return squares[:].rearrange("p k c -> p (k c)")[:, base : base + n]
 
-        def row_sums(k, sq):
+        def row_squares(k0, k1, c0, c1, buf):
+            nc.scalar.activation(
+                out=squares_of(k0, k1, c0, c1, buf).rearrange("p (k c) -> p k c", k=k1 - k0),
+                in_=rows[:, k0:k1, 64 * c0 : 64 * c1],
+                func=ACT.Square,
+            )
+
+        def row_sums(k0, k1, c0, c1, buf):
             nc.vector.tensor_reduce(
-                out=pixel_sq[:, k, :], in_=sq[:].rearrange("p (w c) -> p w c", c=64), axis=AX.X, op=ALU.add
-            )
-            nc.vector.tensor_tensor(
-                out=window_sq[:, k, :], in0=pixel_sq[:, k, 0:32], in1=pixel_sq[:, k, 1:33], op=ALU.add
-            )
-            nc.vector.tensor_tensor(
-                out=window_sq[:, k, :], in0=window_sq[:, k, :], in1=pixel_sq[:, k, 2:34], op=ALU.add
-            )
-            nc.vector.tensor_tensor(
-                out=window_sq[:, k, :], in0=window_sq[:, k, :], in1=pixel_sq[:, k, 3:35], op=ALU.add
+                out=pixel_sq[:, k0:k1, c0:c1],
+                in_=squares_of(k0, k1, c0, c1, buf).rearrange("p (k w c) -> p k w c", k=k1 - k0, c=64),
+                axis=AX.X,
+                op=ALU.add,
             )
 
-        def patch_sums(half):
-            sums = psum.tile([P, 128], F32, tag="turned", bufs=3)
-            for bq in range(4):
-                b = 4 * half + bq
-                k = ROW_TILE_OF[b]
-                n = IMAGE_STARTS.index(35 * b - ROW_TILE_START[k])
+        def window_sums(k0, k1, z0, z1):
+            nc.vector.tensor_tensor(
+                out=two_sq[:, k0:k1, z0 : z1 + 2],
+                in0=pixel_sq[:, k0:k1, z0 : z1 + 2],
+                in1=pixel_sq[:, k0:k1, z0 + 1 : z1 + 3],
+                op=ALU.add,
+            )
+            nc.vector.tensor_tensor(
+                out=window_sq[:, k0:k1, z0:z1],
+                in0=two_sq[:, k0:k1, z0:z1],
+                in1=two_sq[:, k0:k1, z0 + 2 : z1 + 2],
+                op=ALU.add,
+            )
+
+        def patch_sums_into(sums, half, z0, z1):
+            for n, k in enumerate(ROW_TILES_OF[half]):
                 nc.tensor.matmul(
-                    out=sums[:, 32 * bq : 32 * bq + 32],
-                    lhsT=gather[:, n, :, :].rearrange("p i y -> p (i y)"),
-                    rhs=window_sq[:, k, :],
-                    start=True,
-                    stop=True,
+                    out=sums[:, 32 * half + z0 : 32 * half + z1],
+                    lhsT=gather[:, half, n, :],
+                    rhs=window_sq[:, k, z0:z1],
+                    start=(n == 0),
+                    stop=(n == 1),
                 )
+
+        def patch_sums(half, z0, z1):
+            sums = psum.tile([P, 64], F32, tag="turned", bufs=3)
+            patch_sums_into(sums, half, z0, z1)
             return sums
 
-        def patch_norms(half, sums):
-            cols = slice(128 * half, 128 * half + 128)
-            nc.vector.tensor_scalar(out=x_norm[:, cols], in0=sums[:], scalar1=1e-12, scalar2=None, op0=ALU.max)
-            nc.scalar.activation(out=x_norm[:, cols], in_=x_norm[:, cols], func=ACT.Sqrt)
+        def norms_before_root(c0, c1, sums):
             nc.vector.tensor_scalar(
-                out=x_norm[:, cols], in0=x_norm[:, cols], scalar1=qq[:, 0:1], scalar2=None, op0=ALU.add
+                out=x_norm[:, c0:c1], in0=sums[:, c0:c1], scalar1=1e-12, scalar2=None, op0=ALU.max
             )
-            nc.vector.reciprocal(out=x_scale[:, cols], in_=x_norm[:, cols])
 
-        sq0 = row_squares(0)
-        nc.scalar.activation(out=qq[:], in_=q_sb[:], func=ACT.Square, scale=1.0 / 0.3)
-        sq1 = row_squares(1)
-        row_sums(0, sq0)
-        row_sums(1, sq1)
+        def norms_root(c0, c1):
+            nc.scalar.activation(out=x_norm[:, c0:c1], in_=x_norm[:, c0:c1], func=ACT.Sqrt)
+
+        def norms_after_root(c0, c1):
+            nc.vector.tensor_scalar(
+                out=x_norm[:, c0:c1], in0=x_norm[:, c0:c1], scalar1=qq[:, 0:1], scalar2=None, op0=ALU.add
+            )
+            nc.vector.reciprocal(out=x_scale[:, c0:c1], in_=x_norm[:, c0:c1])
 
         live = {}
 
-        def scale(quad):
-            half, z0 = quad // 8, 4 * (quad % 8)
-            scaled = work.tile([P, 4, 4, 256], BF16, tag="scaled")
-            live[("scaled", quad)] = scaled
-            for zi in range(4):
-                for bq in range(4):
-                    b, z = 4 * half + bq, z0 + zi
-                    nc.vector.tensor_scalar(
-                        out=scaled[:, zi, bq, :],
-                        in0=shifted[:, b, 64 * z : 64 * z + 256],
-                        scalar1=x_scale[:, 32 * b + z : 32 * b + z + 1],
-                        scalar2=None,
-                        op0=ALU.mult,
-                    )
+        def scale(n):
+            half, z = n // 32, n % 32
+            if n % 4 == 0:
+                scaled_new = work.tile([P, 4, 1024], BF16, tag="scaled", bufs=2)
+                live[("scaled", n // 4)] = scaled_new
+            nc.vector.tensor_scalar(
+                out=live[("scaled", n // 4)][:, n % 4, :].rearrange("p (i k) -> p i k", i=4),
+                in0=shifted[:, half, :, 64 * z : 64 * z + 256],
+                scalar1=x_scale[:, n : n + 1],
+                scalar2=None,
+                op0=ALU.mult,
+            )
+
+        def transposes(n):
+            scaled = live[("scaled", n // 4)]
+            turned = psum.tile([P, 4, 128], F32, tag="turned", bufs=3)
+            for i in range(4):
+                nc.tensor.transpose(
+                    out=turned[:, i, :], in_=scaled[:, n % 4, 256 * i : 256 * i + 256].bitcast(F32), identity=ident_f[:]
+                )
+            live[("turned", n)] = turned
+
+        def copy_words(on_scalar, words_out, words_in):
+            if on_scalar:
+                nc.scalar.copy(out=words_out, in_=words_in)
+            else:
+                nc.vector.tensor_copy(out=words_out, in_=words_in)
+
+        def leave_psum(n, on_scalar):
+            if n % 4 == 0:
+                grouped_new = work.tile([P, 4, 1024], BF16, tag="grouped", align_bytes=64)
+                live[("grouped", n // 4)] = grouped_new
+            grouped = live[("grouped", n // 4)]
+            copy_words(
+                on_scalar,
+                grouped[:, n % 4, :].bitcast(F32).rearrange("p (g n u) -> p g n u", g=2, u=2),
+                live[("turned", n)][:].rearrange("p (g u) n -> p g n u", u=2),
+            )
+
+        def quantise(n, count):
+            if n % 4 == 0:
+                codes_new = work.tile([P, 1024], U32, tag="codes", align_bytes=64)
+                scales_new = work.tile([P, 1024], U8, tag="scales", align_bytes=64)
+                live[("codes", n // 4)] = (codes_new, scales_new)
+            codes, scales = live[("codes", n // 4)]
+            g0 = n % 4
+            nc.vector.quantize_mx(
+                out=codes[:, 256 * g0 : 256 * (g0 + count)].bitcast(FP8X4),
+                scales=scales[:, 256 * g0 : 256 * (g0 + count)],
+                in_=live[("grouped", n // 4)][:, g0 : g0 + count, :].rearrange("p z n -> p (z n)"),
+            )
 
         w_norm = const.tile([P, 4], F32)
-        for ub in range(4):
-            w_turned = psum.tile([P, 8, 128], BF16, tag="acc", bufs=4)
+        w_scale = const.tile([P, 4], F32)
+        unused = epi.tile([P, 1024], BF16, tag="sign")
+        w_scaled = work.tile([P, 4, 1024], BF16, tag="scaled", bufs=2)
+        w_grouped = work.tile([P, 2, 512, 4], BF16, tag="grouped", align_bytes=64)
+        w_words = w_grouped[:].rearrange("p g n t -> p g (n t)").bitcast(F32).rearrange("p g (n u) -> p g n u", u=2)
+        w_turned = []
+        w_back = []
+
+        def w_transposes(ub):
+            w_turned_ub = psum.tile([P, 8, 128], BF16, tag="acc", bufs=4)
+            w_turned.append(w_turned_ub)
             for s in range(8):
                 nc.tensor.transpose(
-                    out=w_turned[:, s, :], in_=w_raw[:, s, 128 * ub : 128 * ub + 128], identity=ident_bf[:]
+                    out=w_turned_ub[:, s, :], in_=w_raw[s // 4][:, s % 4, 128 * ub : 128 * ub + 128], identity=ident_bf[:]
                 )
-            unused = epi.tile([P, 1024], BF16, tag="sign")
+
+        def w_squares(ub):
             nc.scalar.activation(
                 out=unused[:],
-                in_=w_turned[:].rearrange("p s k -> p (s k)"),
+                in_=w_turned[ub][:].rearrange("p s k -> p (s k)"),
                 func=ACT.Square,
                 accum_out=w_norm[:, ub : ub + 1],
             )
-        sums0 = patch_sums(0)
-        nc.vector.tensor_scalar(out=w_norm[:], in0=w_norm[:], scalar1=1e-12, scalar2=None, op0=ALU.max)
-        nc.scalar.activation(out=w_norm[:], in_=w_norm[:], func=ACT.Sqrt)
-        nc.vector.tensor_scalar(out=w_norm[:], in0=w_norm[:], scalar1=qq[:, 0:1], scalar2=None, op0=ALU.add)
-        w_scale_col = const.tile([P, 4], F32)
-        nc.vector.reciprocal(out=w_scale_col[:], in_=w_norm[:])
-        patch_norms(0, sums0)
-        w_scale = psum.tile([P, 512], F32, tag="acc", bufs=4)
+
+        def w_norms(u0, u1):
+            cols = slice(u0, u1)
+            nc.vector.tensor_scalar(out=w_norm[:, cols], in0=w_norm[:, cols], scalar1=1e-12, scalar2=None, op0=ALU.max)
+            nc.scalar.activation(out=w_norm[:, cols], in_=w_norm[:, cols], func=ACT.Sqrt)
+            nc.vector.tensor_scalar(
+                out=w_norm[:, cols], in0=w_norm[:, cols], scalar1=qq[:, 0:1], scalar2=None, op0=ALU.add
+            )
+            nc.vector.reciprocal(out=w_scale[:, cols], in_=w_norm[:, cols])
+
+        def w_times_scale(ub, on_scalar):
+            w_turned_ub = w_turned[ub][:].rearrange("p s k -> p (s k)")
+            factor = w_scale[:, ub : ub + 1]
+            if on_scalar:
+                nc.scalar.activation(out=w_scaled[:, ub, :], in_=w_turned_ub, func=ACT.Copy, scale=factor)
+            else:
+                nc.vector.tensor_scalar(
+                    out=w_scaled[:, ub, :], in0=w_turned_ub, scalar1=factor, scalar2=None, op0=ALU.mult
+                )
+
+        def w_transposes_back(ub):
+            w_back_ub = psum.tile([P, 4, 128], F32, tag="acc", bufs=4)
+            w_back.append(w_back_ub)
+            for i in range(4):
+                nc.tensor.transpose(
+                    out=w_back_ub[:, i, :], in_=w_scaled[:, ub, 256 * i : 256 * i + 256].bitcast(F32), identity=ident_f[:]
+                )
+
+        def w_leave_psum(ub, on_scalar):
+            copy_words(on_scalar, w_words[:, :, 128 * ub : 128 * ub + 128, :], w_back[ub][:].rearrange("p (g u) n -> p g n u", u=2))
+
+        expo = psum.tile([P, 512], F32, tag="expo", bufs=1)
+        nc.scalar.activation(out=expo_row[0:1, :], in_=p_row[:], func=ACT.Square, scale=0.2)
+        nc.tensor.matmul(out=expo[:], lhsT=ones_f[:], rhs=expo_row[:], start=True, stop=True)
+        expo_sb = const.tile([P, 512], F32)
+        row_squares(0, 2, 0, FIRST_PIXELS, 0)
+        row_sums(0, 2, 0, FIRST_PIXELS, 0)
+        window_sums(0, 2, 0, FIRST_Z)
         for ub in range(4):
-            nc.tensor.matmul(
-                out=w_scale[:, 128 * ub : 128 * ub + 128],
-                lhsT=w_scale_col[:, ub : ub + 1].to_broadcast([P, P]),
-                rhs=ident_f[:],
-                start=True,
-                stop=True,
-            )
+            w_transposes(ub)
+        w_squares(0)
+        w_squares(1)
+        sums_a = patch_sums(0, 0, FIRST_Z)
+        norms_before_root(0, FIRST_Z, sums_a)
+        norms_root(0, FIRST_Z)
+        w_norms(0, 2)
+        norms_after_root(0, FIRST_Z)
+        w_squares(2)
+        w_squares(3)
+        w_times_scale(0, False)
+        w_times_scale(1, False)
         scale(0)
-        w_grouped = epi.tile([P, 2, 512, 4], BF16, tag="value", align_bytes=64)
-        w_tg = w_raw[:].rearrange("p (t g) n -> p t g n", g=2)
-        for g in range(2):
-            nc.vector.tensor_tensor(
-                out=w_grouped[:, g, :, :],
-                in0=w_tg[:, :, g, :].rearrange("p t n -> p n t"),
-                in1=w_scale[:].unsqueeze(2).to_broadcast([P, 512, 4]),
-                op=ALU.mult,
-            )
+        scale(1)
+        w_transposes_back(0)
+        w_transposes_back(1)
+        transposes(0)
+        transposes(1)
+        w_norms(2, 4)
+        scale(2)
+        scale(3)
+        w_leave_psum(0, True)
+        w_times_scale(2, False)
+        w_times_scale(3, True)
+        w_leave_psum(1, False)
+        w_transposes_back(2)
+        w_transposes_back(3)
+        transposes(2)
+        leave_psum(0, True)
+        leave_psum(1, True)
+        w_leave_psum(2, False)
+        w_leave_psum(3, True)
+        transposes(3)
+        leave_psum(2, True)
+        quantise(0, 2)
         w_codes = const.tile([P, 1024], U32, align_bytes=64)
         w_scales = const.tile([P, 1024], U8, align_bytes=64)
         nc.vector.quantize_mx(
-            out=w_codes[:].bitcast(FP8X4),
-            scales=w_scales[:],
-            in_=w_grouped[:].rearrange("p g n t -> p (g n t)"),
+            out=w_codes[:].bitcast(FP8X4), scales=w_scales[:], in_=w_grouped[:].rearrange("p g n t -> p (g n t)")
         )
-
-        expo = psum.tile([P, 512], F32, tag="expo", bufs=1)
+        leave_psum(3, True)
+        for n in range(4, 8):
+            scale(n)
+        quantise(2, 2)
         out_v = out.rearrange("b y z u -> (b y) z u")
 
-        def transposes(n):
-            quad, zi = n // 4, n % 4
-            scaled = live[("scaled", quad)]
-            turned = psum.tile([P, 2, 4, 128], BF16, tag="turned", bufs=3)
-            for g in range(2):
-                for bq in range(4):
-                    nc.tensor.transpose(
-                        out=turned[:, g, bq, :], in_=scaled[:, zi, bq, 128 * g : 128 * g + 128], identity=perm[:]
-                    )
-            live[("turned", n)] = turned
-
-        def leave_psum(n, engine_is_scalar):
-            quad, zi = n // 4, n % 4
-            if zi == 0:
-                grouped_new = work.tile([P, 4, 1024], BF16, tag="grouped", align_bytes=64)
-                live[("grouped", quad)] = grouped_new
-            grouped = live[("grouped", quad)]
-            turned = live[("turned", n)][:].rearrange("p g b n -> p (g b n)")
-            if engine_is_scalar:
-                nc.scalar.copy(out=grouped[:, zi, :], in_=turned)
-            else:
-                nc.vector.tensor_copy(out=grouped[:, zi, :], in_=turned)
-
-        def quantise(quad):
-            codes = work.tile([P, 1024], U32, tag="codes", align_bytes=64)
-            scales = work.tile([P, 1024], U8, tag="scales", align_bytes=64)
-            nc.vector.quantize_mx(
-                out=codes[:].bitcast(FP8X4),
-                scales=scales[:],
-                in_=live[("grouped", quad)][:].rearrange("p z n -> p (z n)"),
-            )
-            live[("codes", quad)] = (codes, scales)
-
         def multiply(n):
-            quad, zi = n // 4, n % 4
-            codes, scales = live[("codes", quad)]
+            codes, scales = live[("codes", n // 4)]
             acc = psum.tile([P, 512], F32, tag="acc", bufs=4)
             for g in range(2):
-                c0 = 256 * zi + 128 * g
+                c0 = 256 * (n % 4) + 128 * g
                 nc.tensor.matmul_mx(
                     out=acc[:],
                     lhsT=codes[:, c0 : c0 + 128].bitcast(FP8X4),
@@ -272,104 +355,130 @@ def tile_cossim2d_t_kernel(tc, x, w, p, q, out):
                 )
             live[("acc", n)] = acc
 
-        def sign_and_abs(n):
-            quad, zi = n // 4, n % 4
-            if zi == 0:
-                sign_new = epi.tile([P, 4, 512], BF16, tag="sign")
-                value_new = epi.tile([P, 4, 512], F32, tag="value", align_bytes=64)
-                live[("sign", quad)] = sign_new
-                live[("value", quad)] = value_new
-            acc = live[("acc", n)]
-            sign = live[("sign", quad)][:, zi, :]
-            nc.scalar.activation(out=sign, in_=acc[:], func=ACT.Sign)
-            nc.vector.tensor_tensor(out=live[("value", quad)][:, zi, :], in0=acc[:], in1=sign, op=ALU.mult)
+        def take_sign(n):
+            if n % 2 == 0:
+                sign_new = epi.tile([P, 2, 512], BF16, tag="sign")
+                value_new = epi.tile([P, 2, 512], F32, tag="value")
+                live[("sign", n // 2)] = sign_new
+                live[("value", n // 2)] = value_new
+            nc.scalar.activation(out=live[("sign", n // 2)][:, n % 2, :], in_=live[("acc", n)][:], func=ACT.Sign)
+
+        def take_abs(n):
+            nc.vector.tensor_tensor(out=value(n), in0=live[("acc", n)][:], in1=sign(n), op=ALU.mult)
 
         def value(n):
-            return live[("value", n // 4)][:, n % 4, :]
+            return live[("value", n // 2)][:, n % 2, :]
+
+        def sign(n):
+            return live[("sign", n // 2)][:, n % 2, :]
 
         def store(n, count):
             half, z = n // 32, n % 32
             nc.sync.dma_start(
                 out=out_v[128 * half : 128 * half + 128, z : z + count, :],
-                in_=live[("value", n // 4)][:, n % 4 : n % 4 + count, :],
+                in_=live[("value", n // 2)][:, n % 2 : n % 2 + count, :],
             )
 
         long_work = []
-        for chunk in CHUNKS:
-            for func in (ACT.Ln, ACT.Exp):
-                long_work.extend([(func, 4 * quad + zi) for quad in chunk for zi in range(4)])
-        done = [0, 0, 0]
-        logs, powers = [], []
-        multiplied = {}
+        start_of = 0
+        for c, chunk in enumerate(CHUNKS):
+            for ph, func in enumerate((ACT.Ln, ACT.Exp)):
+                for n in range(start_of, start_of + chunk, 2):
+                    long_work.append((func, n, 2 * c + ph))
+            start_of += chunk
+        done = {"long": 0, "mult": 0, "sign": 0}
+        abs_at, log_at, mult_at, power_at = {}, {}, {}, {}
 
-        def next_is_ln():
-            return done[0] >= len(long_work) or long_work[done[0]][0] == ACT.Ln
+        def phase():
+            return long_work[min(done["long"], len(long_work) - 1)][2]
 
         def long_piece(step):
-            if done[0] >= len(long_work):
+            if done["long"] >= len(long_work):
                 return
-            func, n = long_work[done[0]]
-            if func == ACT.Ln and n + 3 + LN_LAG <= step:
-                nc.scalar.activation(out=value(n), in_=value(n), func=ACT.Ln, bias=eps_t[:, 0:1])
-                logs.append((n, step))
-                done[0] += 1
-            elif func == ACT.Exp and multiplied.get(n, step) + NEXT_LAG <= step:
-                nc.scalar.activation(out=value(n), in_=value(n), func=ACT.Exp)
-                powers.append((n, step))
-                done[0] += 1
+            func, n, ph = long_work[done["long"]]
+            v = live.get(("value", n // 2))
+            if func == ACT.Ln and step > NORM_END + 1 and abs_at.get(n + 1, step) + 1 <= step:
+                nc.scalar.activation(out=v[:], in_=v[:], func=ACT.Ln, bias=eps_t[:, 0:1])
+                log_at[n] = step
+                log_at[n + 1] = step
+                done["long"] += 1
+            elif func == ACT.Exp and max(mult_at.get(n, step), mult_at.get(n + 1, step)) + 1 <= step:
+                nc.scalar.activation(out=v[:], in_=v[:], func=ACT.Exp)
+                power_at[n] = step
+                power_at[n + 1] = step
+                done["long"] += 1
+
+        def on_gpsimd(n):
+            ph = 0 if n < CHUNKS[0] else 2
+            return GPSIMD_EXPO[ph][n % 4]
 
         def times_exponent(step):
-            if done[1] < len(logs) and logs[done[1]][1] + NEXT_LAG <= step:
-                n = logs[done[1]][0]
-                nc.vector.tensor_tensor(out=value(n), in0=value(n), in1=expo[:], op=ALU.mult)
-                multiplied[n] = step
-                done[1] += 1
+            n = done["mult"]
+            if n < GROUPS and log_at.get(n, step) + 1 <= step:
+                if on_gpsimd(n):
+                    nc.gpsimd.tensor_tensor(out=value(n), in0=value(n), in1=expo_sb[:], op=ALU.mult)
+                else:
+                    nc.vector.tensor_tensor(out=value(n), in0=value(n), in1=expo[:], op=ALU.mult)
+                mult_at[n] = step
+                done["mult"] += 1
 
         def times_sign(step, engine):
-            if done[2] < len(powers) and powers[done[2]][1] + NEXT_LAG <= step:
-                n = powers[done[2]][0]
-                engine.tensor_tensor(out=value(n), in0=value(n), in1=live[("sign", n // 4)][:, n % 4, :], op=ALU.mult)
-                if n // 4 >= FIRST_FINE_STORE:
+            n = done["sign"]
+            if n < GROUPS and power_at.get(n, step) + 1 <= step:
+                engine.tensor_tensor(out=value(n), in0=value(n), in1=sign(n), op=ALU.mult)
+                if n >= GROUPS - 8:
                     store(n, 1)
-                elif n % 4 == 3:
-                    store(n - 3, 4)
-                done[2] += 1
+                elif n % 2 == 1:
+                    store(n - 1, 2)
+                done["sign"] += 1
 
-        scale(1)
-        for step in range(-4, 4 * GROUPS):
-            if done[0] >= len(long_work) and done[2] >= len(powers):
+        for step in range(4 - LEAD, 4 * GROUPS):
+            if done["sign"] >= GROUPS:
                 break
-            drained = step > GROUPS + 3
-            if step == 5:
-                nc.scalar.activation(out=expo_row[0:1, :], in_=p_row[:], func=ACT.Square, scale=0.2)
-            if step == 6:
-                nc.tensor.matmul(out=expo[:], lhsT=ones_f[:], rhs=expo_row[:], start=True, stop=True)
-            if step == 2:
-                live["sq2"] = row_squares(2)
-            if step == 3:
-                row_sums(2, live["sq2"])
-            if step == 4:
-                patch_norms(1, patch_sums(1))
-            if step % 4 == 1 and 0 <= step // 4 < QUADS:
-                quantise(step // 4)
-                if step // 4 + 2 < QUADS:
-                    scale(step // 4 + 2)
+            drained = step >= GROUPS + 2
+            if step == 0:
+                nc.vector.tensor_copy(out=expo_sb[:], in_=expo[:])
+            for job, (k0, k1, c0, c1, first_step) in enumerate(NORM_JOBS):
+                if step == first_step:
+                    row_squares(k0, k1, c0, c1, job % 2)
+                if step == first_step + 1:
+                    row_sums(k0, k1, c0, c1, job % 2)
+            if step == NORM_END:
+                window_sums(0, 2, FIRST_Z, 32)
+                window_sums(2, 3, 0, 32)
+            if step == NORM_END + 1:
+                live["sums"] = patch_sums(0, FIRST_Z, 32)
+                patch_sums_into(live["sums"], 1, 0, 32)
+                norms_before_root(FIRST_Z, 64, live["sums"])
+                norms_root(FIRST_Z, 64)
+            if step == NORM_END + 2:
+                norms_after_root(FIRST_Z, 64)
+            ahead = step + 1
+            if ahead % 4 == 0 and 0 <= ahead < GROUPS:
+                if ahead > 0:
+                    quantise(ahead, 4)
+                if ahead + 8 < GROUPS:
+                    for n in range(ahead + 8, ahead + 12):
+                        scale(n)
+            if 0 <= step < GROUPS:
+                multiply(step)
+            if 4 <= step + LEAD < GROUPS:
+                transposes(step + LEAD)
+            if 0 <= step - 1 < GROUPS:
+                take_sign(step - 1)
+            if 4 <= step + LEAD - 1 < GROUPS:
+                leave_psum(step + LEAD - 1, SCALAR_COPIES[phase()][step % 4])
+            long_piece(step)
             if 0 <= step - 2 < GROUPS:
-                multiply(step - 2)
-            if 0 <= step + 4 < GROUPS:
-                transposes(step + 4)
-            long_piece(step)
-            if 0 <= step - 3 < GROUPS:
-                sign_and_abs(step - 3)
-            if 0 <= step + 3 < GROUPS:
-                leave_psum(step + 3, next_is_ln())
-            long_piece(step)
+                take_abs(step - 2)
+                abs_at[step - 2] = step
             for repeat in range(4 if drained else 2):
                 times_exponent(step)
-            for repeat in range(4 if drained else 1):
-                times_sign(step, nc.vector if drained else nc.gpsimd)
             if drained:
-                long_piece(step)
-                times_exponent(step)
                 times_sign(step, nc.vector)
-        assert done[0] == len(long_work) and done[2] == len(powers)
+                times_sign(step, nc.vector)
+            else:
+                times_sign(step, nc.gpsimd)
+                if step % 2 == 0:
+                    times_sign(step, nc.gpsimd)
+        assert done["sign"] == GROUPS and done["long"] == len(long_work)

@@ -24,11 +24,18 @@ ROW_TILES_OF = ((0, 1), (1, 2))
 FIRST_PIXELS = 19
 FIRST_Z = FIRST_PIXELS - 3
 CHUNKS = (32, 32)
+LN_LAG = 3
+MULT_LAG = 1
 LEAD = 7
-SCALAR_COPIES = ((1, 1, 1, 0), (0, 0, 0, 0), (0, 1, 0, 1), (0, 0, 0, 0))
-GPSIMD_EXPO = ((0, 1, 0, 1), (0, 0, 0, 0), (0, 0, 0, 0), (0, 0, 0, 0))
+COPIES_ON_SCALAR = (5, 0, 3, 0)
+EXPO_ON_GPSIMD = (4, 2)
+SIGN_ON_GPSIMD = 32
 NORM_JOBS = ((0, 2, 19, 27, -2), (0, 2, 27, 35, -1), (2, 3, 0, 18, 0), (2, 3, 18, 35, 1))
 NORM_END = 3
+
+
+def spread(n, share):
+    return (n + 1) * share // 8 > n * share // 8
 
 
 def tile_cossim2d_t_kernel(tc, x, w, p, q, out):
@@ -76,11 +83,10 @@ def tile_cossim2d_t_kernel(tc, x, w, p, q, out):
         load_shifted(1, 0, 35)
 
         eps_t = const.tile([P, 1], F32)
-        nc.vector.memset(eps_t[:], 1.0)
-        warm = const.tile([P, 1], F32)
-        nc.scalar.activation(out=warm[:], in_=eps_t[:], func=ACT.Sqrt)
-        nc.vector.memset(eps_t[:], 0.0)
-        nc.vector.tensor_scalar(out=eps_t[:], in0=eps_t[:], scalar1=1e-6, scalar2=None, op0=ALU.add)
+        warm = const.tile([P, 2], F32)
+        nc.vector.memset(warm[:], 0.0)
+        nc.scalar.activation(out=warm[:, 1:2], in_=warm[:, 0:1], func=ACT.Sqrt)
+        nc.vector.tensor_scalar(out=eps_t[:], in0=warm[:, 0:1], scalar1=1e-6, scalar2=None, op0=ALU.add)
         ident_f = const.tile([P, P], F32)
         make_identity(nc, ident_f[:])
         ident_bf = const.tile([P, P], BF16)
@@ -364,7 +370,7 @@ def tile_cossim2d_t_kernel(tc, x, w, p, q, out):
             nc.scalar.activation(out=live[("sign", n // 2)][:, n % 2, :], in_=live[("acc", n)][:], func=ACT.Sign)
 
         def take_abs(n):
-            nc.vector.tensor_tensor(out=value(n), in0=live[("acc", n)][:], in1=sign(n), op=ALU.mult)
+            nc.vector.tensor_tensor(out=value(n), in0=sign(n), in1=live[("acc", n)][:], op=ALU.mult)
 
         def value(n):
             return live[("value", n // 2)][:, n % 2, :]
@@ -397,7 +403,7 @@ def tile_cossim2d_t_kernel(tc, x, w, p, q, out):
                 return
             func, n, ph = long_work[done["long"]]
             v = live.get(("value", n // 2))
-            if func == ACT.Ln and step > NORM_END + 1 and abs_at.get(n + 1, step) + 1 <= step:
+            if func == ACT.Ln and step > NORM_END + 1 and abs_at.get(n + 1, step) + LN_LAG <= step:
                 nc.scalar.activation(out=v[:], in_=v[:], func=ACT.Ln, bias=eps_t[:, 0:1])
                 log_at[n] = step
                 log_at[n + 1] = step
@@ -408,29 +414,37 @@ def tile_cossim2d_t_kernel(tc, x, w, p, q, out):
                 power_at[n + 1] = step
                 done["long"] += 1
 
-        def on_gpsimd(n):
-            ph = 0 if n < CHUNKS[0] else 2
-            return GPSIMD_EXPO[ph][n % 4]
+        def on_gpsimd(m):
+            if 2 * m < CHUNKS[0]:
+                return spread(m, EXPO_ON_GPSIMD[0])
+            return m - CHUNKS[0] // 2 < EXPO_ON_GPSIMD[1]
 
         def times_exponent(step):
             n = done["mult"]
-            if n < GROUPS and log_at.get(n, step) + 1 <= step:
-                if on_gpsimd(n):
-                    nc.gpsimd.tensor_tensor(out=value(n), in0=value(n), in1=expo_sb[:], op=ALU.mult)
+            if n < GROUPS and log_at.get(n, step) + MULT_LAG <= step:
+                if on_gpsimd(n // 2):
+                    for k in (n, n + 1):
+                        nc.gpsimd.tensor_tensor(out=value(k), in0=value(k), in1=expo_sb[:], op=ALU.mult)
                 else:
-                    nc.vector.tensor_tensor(out=value(n), in0=value(n), in1=expo[:], op=ALU.mult)
+                    v = live[("value", n // 2)]
+                    nc.vector.tensor_tensor(
+                        out=v[:], in0=v[:], in1=expo[:].unsqueeze(1).to_broadcast([P, 2, 512]), op=ALU.mult
+                    )
                 mult_at[n] = step
-                done["mult"] += 1
+                mult_at[n + 1] = step
+                done["mult"] += 2
 
-        def times_sign(step, engine):
+        def times_sign(step):
             n = done["sign"]
             if n < GROUPS and power_at.get(n, step) + 1 <= step:
-                engine.tensor_tensor(out=value(n), in0=value(n), in1=sign(n), op=ALU.mult)
-                if n >= GROUPS - 8:
-                    store(n, 1)
-                elif n % 2 == 1:
-                    store(n - 1, 2)
-                done["sign"] += 1
+                v, s = live[("value", n // 2)], live[("sign", n // 2)]
+                if n < SIGN_ON_GPSIMD:
+                    for k in range(2):
+                        nc.gpsimd.tensor_tensor(out=v[:, k, :], in0=v[:, k, :], in1=s[:, k, :], op=ALU.mult)
+                else:
+                    nc.vector.tensor_tensor(out=v[:], in0=v[:], in1=s[:], op=ALU.mult)
+                store(n, 2)
+                done["sign"] += 2
 
         for step in range(4 - LEAD, 4 * GROUPS):
             if done["sign"] >= GROUPS:
@@ -467,18 +481,13 @@ def tile_cossim2d_t_kernel(tc, x, w, p, q, out):
             if 0 <= step - 1 < GROUPS:
                 take_sign(step - 1)
             if 4 <= step + LEAD - 1 < GROUPS:
-                leave_psum(step + LEAD - 1, SCALAR_COPIES[phase()][step % 4])
+                leave_psum(step + LEAD - 1, spread(step + LEAD - 1, COPIES_ON_SCALAR[phase()]))
             long_piece(step)
             if 0 <= step - 2 < GROUPS:
                 take_abs(step - 2)
                 abs_at[step - 2] = step
-            for repeat in range(4 if drained else 2):
+            for repeat in range(2):
                 times_exponent(step)
-            if drained:
-                times_sign(step, nc.vector)
-                times_sign(step, nc.vector)
-            else:
-                times_sign(step, nc.gpsimd)
-                if step % 2 == 0:
-                    times_sign(step, nc.gpsimd)
+            for repeat in range(2):
+                times_sign(step)
         assert done["sign"] == GROUPS and done["long"] == len(long_work)

@@ -1,3 +1,4 @@
+import math
 from contextlib import ExitStack
 
 import concourse.mybir as mybir
@@ -27,6 +28,7 @@ CHUNKS = (32, 32)
 LN_LAG = 3
 MULT_LAG = 1
 LEAD = 7
+TINY = 2.0**-100
 COPIES_ON_SCALAR = (5, 0, 3, 0)
 EXPO_ON_GPSIMD = (4, 2)
 SIGN_ON_GPSIMD = 32
@@ -72,7 +74,7 @@ def tile_cossim2d_t_kernel(tc, x, w, p, q, out):
         w_rows = w.rearrange("o (s r) n -> r (o s) n", r=P)
         w_raw = []
         for h in range(2):
-            w_raw_h = epi.tile([P, 4, 512], BF16, tag="value", name="w_raw%d" % h)
+            w_raw_h = epi.tile([P, 4, 512], BF16, tag="value", name="w_raw%d" % h, bufs=21)
             nc.sync.dma_start(out=w_raw_h[:], in_=w_rows[:, 4 * h : 4 * h + 4, :])
             w_raw.append(w_raw_h)
         load_shifted(0, 0, FIRST_PIXELS)
@@ -87,6 +89,10 @@ def tile_cossim2d_t_kernel(tc, x, w, p, q, out):
         nc.vector.memset(warm[:], 0.0)
         nc.scalar.activation(out=warm[:, 1:2], in_=warm[:, 0:1], func=ACT.Sqrt)
         nc.vector.tensor_scalar(out=eps_t[:], in0=warm[:, 0:1], scalar1=1e-6, scalar2=None, op0=ALU.add)
+        shift_t = const.tile([P, 1], F32)
+        nc.vector.tensor_scalar(
+            out=shift_t[:], in0=warm[:, 0:1], scalar1=-math.log(TINY), scalar2=None, op0=ALU.add
+        )
         ident_f = const.tile([P, P], F32)
         make_identity(nc, ident_f[:])
         ident_bf = const.tile([P, P], BF16)
@@ -238,7 +244,7 @@ def tile_cossim2d_t_kernel(tc, x, w, p, q, out):
 
         w_norm = const.tile([P, 4], F32)
         w_scale = const.tile([P, 4], F32)
-        unused = epi.tile([P, 1024], BF16, tag="sign")
+        unused = epi.tile([P, 1024], BF16, tag="sign", bufs=19)
         w_scaled = work.tile([P, 4, 1024], BF16, tag="scaled", bufs=2)
         w_grouped = work.tile([P, 2, 512, 4], BF16, tag="grouped", align_bytes=64)
         w_words = w_grouped[:].rearrange("p g n t -> p g (n t)").bitcast(F32).rearrange("p g (n u) -> p g n u", u=2)
@@ -363,14 +369,17 @@ def tile_cossim2d_t_kernel(tc, x, w, p, q, out):
 
         def take_sign(n):
             if n % 2 == 0:
-                sign_new = epi.tile([P, 2, 512], BF16, tag="sign")
-                value_new = epi.tile([P, 2, 512], F32, tag="value")
-                live[("sign", n // 2)] = sign_new
+                value_new = epi.tile([P, 2, 512], F32, tag="value", bufs=21)
                 live[("value", n // 2)] = value_new
-            nc.scalar.activation(out=live[("sign", n // 2)][:, n % 2, :], in_=live[("acc", n)][:], func=ACT.Sign)
+            nc.scalar.activation(out=value(n), in_=live[("acc", n)][:], func=ACT.Abs)
 
         def take_abs(n):
-            nc.vector.tensor_tensor(out=value(n), in0=sign(n), in1=live[("acc", n)][:], op=ALU.mult)
+            if n % 2 == 0:
+                sign_new = epi.tile([P, 2, 512], BF16, tag="sign", bufs=19)
+                live[("sign", n // 2)] = sign_new
+            nc.vector.tensor_scalar(
+                out=sign(n), in0=live[("acc", n)][:], scalar1=-TINY, scalar2=TINY, op0=ALU.max, op1=ALU.min
+            )
 
         def value(n):
             return live[("value", n // 2)][:, n % 2, :]
@@ -409,7 +418,7 @@ def tile_cossim2d_t_kernel(tc, x, w, p, q, out):
                 log_at[n + 1] = step
                 done["long"] += 1
             elif func == ACT.Exp and max(mult_at.get(n, step), mult_at.get(n + 1, step)) + 1 <= step:
-                nc.scalar.activation(out=v[:], in_=v[:], func=ACT.Exp)
+                nc.scalar.activation(out=v[:], in_=v[:], func=ACT.Exp, bias=shift_t[:, 0:1])
                 power_at[n] = step
                 power_at[n + 1] = step
                 done["long"] += 1

import math
from contextlib import ExitStack

import concourse.mybir as mybir
from concourse.masks import make_identity

F32 = mybir.dt.float32
BF16 = mybir.dt.bfloat16
U32 = mybir.dt.uint32
U8 = mybir.dt.uint8
FP8X4 = mybir.dt.float8_e4m3fn_x4
ACT = mybir.ActivationFunctionType
ALU = mybir.AluOpType
AX = mybir.AxisListType

FLOPS = 2 * 8192 * 1024 * 512

P = 128
ROW = 35 * 64
GROUPS = 64
QUADS = 16
ROW_TILE_START = (0, 105, 152)
IMAGE_AT = ((0, 0, 0, 0), (0, 1, 0, 35), (0, 2, 0, 70), (0, 3, 1, 0), (1, 0, 1, 35), (1, 1, 1, 70), (1, 2, 2, 58), (1, 3, 2, 93))
ROW_TILES_OF = ((0, 1), (1, 2))
FIRST_PIXELS = 19
FIRST_Z = FIRST_PIXELS - 3
CHUNKS = (32, 32)
LN_LAG = 3
MULT_LAG = 1
LEAD = 7
TINY = 2.0**-100
COPIES_ON_SCALAR = (5, 0, 3, 0)
EXPO_ON_GPSIMD = (4, 2)
SIGN_ON_GPSIMD = 32
NORM_JOBS = ((0, 2, 19, 27, -2), (0, 2, 27, 35, -1), (2, 3, 0, 18, 0), (2, 3, 18, 35, 1))
NORM_END = 3


def spread(n, share):
    return (n + 1) * share // 8 > n * share // 8


def tile_cossim2d_t_kernel(tc, x, w, p, q, out):
    nc = tc.nc
    with ExitStack() as ctx:
        const = ctx.enter_context(tc.tile_pool(name="const", bufs=1))
        work = ctx.enter_context(tc.tile_pool(name="work", bufs=2))
        epi = ctx.enter_context(tc.tile_pool(name="epi", bufs=20))
        psum = ctx.enter_context(tc.psum_pool(name="psum", bufs=4))
        ctx.enter_context(tc.manual_schedule())

        x_rows = x.rearrange("b h w c -> (b h) (w c)")
        rows = const.tile([P, 3, ROW], BF16)
        shifted = const.tile([P, 2, 4, ROW], BF16)

        def load_rows(k, c0, c1):
            r0 = ROW_TILE_START[k]
            nc.sync.dma_start(out=rows[:, k, 64 * c0 : 64 * c1], in_=x_rows[r0 : r0 + 128, 64 * c0 : 64 * c1])

        def load_shifted(half, c0, c1):
            for i in range(4):
                for bq in (0, 2, 1, 3):
                    nc.sync.dma_start(
                        out=shifted[32 * bq : 32 * bq + 32, half, i, 64 * c0 : 64 * c1],
                        in_=x[4 * half + bq, i : i + 32, c0:c1, :].rearrange("y w c -> y (w c)"),
                    )

        q_sb = const.tile([P, 1], BF16)
        nc.scalar.dma_start(out=q_sb[:], in_=q.partition_broadcast(P))
        p_row = const.tile([1, 512], BF16)
        nc.scalar.dma_start(out=p_row[:], in_=p.unsqueeze(0))
        load_rows(0, 0, FIRST_PIXELS)
        load_rows(1, 0, FIRST_PIXELS)
        w_rows = w.rearrange("o (s r) n -> r (o s) n", r=P)
        w_raw = []
        for h in range(2):
            w_raw_h = epi.tile([P, 4, 512], BF16, tag="value", name="w_raw%d" % h, bufs=21)
            nc.sync.dma_start(out=w_raw_h[:], in_=w_rows[:, 4 * h : 4 * h + 4, :])
            w_raw.append(w_raw_h)
        load_shifted(0, 0, FIRST_PIXELS)
        load_rows(0, FIRST_PIXELS, 35)
        load_rows(1, FIRST_PIXELS, 35)
        load_shifted(0, FIRST_PIXELS, 35)
        load_rows(2, 0, 35)
        load_shifted(1, 0, 35)

        eps_t = const.tile([P, 1], F32)
        warm = const.tile([P, 2], F32)
        nc.vector.memset(warm[:], 0.0)
        nc.scalar.activation(out=warm[:, 1:2], in_=warm[:, 0:1], func=ACT.Sqrt)
        nc.vector.tensor_scalar(out=eps_t[:], in0=warm[:, 0:1], scalar1=1e-6, scalar2=None, op0=ALU.add)
        shift_t = const.tile([P, 1], F32)
        nc.vector.tensor_scalar(
            out=shift_t[:], in0=warm[:, 0:1], scalar1=-math.log(TINY), scalar2=None, op0=ALU.add
        )
        ident_f = const.tile([P, P], F32)
        make_identity(nc, ident_f[:])
        ident_bf = const.tile([P, P], BF16)
        nc.vector.tensor_copy(out=ident_bf[:], in_=ident_f[:])
        ones_f = const.tile([P, P], F32)
        nc.vector.memset(ones_f[:], 1.0)
        expo_row = const.tile([P, 512], F32)
        nc.vector.memset(expo_row[:], 0.0)
        ident_wide = const.tile([P, 132], F32)
        nc.vector.memset(ident_wide[:], 0.0)
        nc.vector.tensor_copy(out=ident_wide[:, 0:128], in_=ident_f[:])
        pairs = const.tile([P, 130], F32)
        nc.vector.tensor_tensor(out=pairs[:], in0=ident_wide[:, 0:130], in1=ident_wide[:, 1:131], op=ALU.add)
        band = const.tile([P, 128], F32)
        nc.vector.tensor_tensor(out=band[:], in0=pairs[:, 0:128], in1=pairs[:, 2:130], op=ALU.add)
        gather = const.tile([P, 2, 2, 128], F32)
        nc.vector.memset(gather[:], 0.0)
        for half, bq, k, start in IMAGE_AT:
            nc.vector.tensor_copy(
                out=gather[:, half, ROW_TILES_OF[half].index(k), 32 * bq : 32 * bq + 32],
                in_=band[:, start : start + 32],
            )

        squares = const.tile([P, 2, 64 * FIRST_PIXELS], F32)
        pixel_sq = const.tile([P, 3, 35], F32)
        two_sq = const.tile([P, 3, 34], F32)
        window_sq = const.tile([P, 3, 32], F32)
        qq = const.tile([P, 1], F32)
        x_norm = const.tile([P, 64], F32)
        x_scale = const.tile([P, 64], F32)
        nc.scalar.activation(out=qq[:], in_=q_sb[:], func=ACT.Square, scale=1.0 / 0.3)

        def squares_of(k0, k1, c0, c1, buf):
            n = (k1 - k0) * (c1 - c0) * 64
            base = buf * 64 * FIRST_PIXELS
            return squares[:].rearrange("p k c -> p (k c)")[:, base : base + n]

        def row_squares(k0, k1, c0, c1, buf):
            nc.scalar.activation(
                out=squares_of(k0, k1, c0, c1, buf).rearrange("p (k c) -> p k c", k=k1 - k0),
                in_=rows[:, k0:k1, 64 * c0 : 64 * c1],
                func=ACT.Square,
            )

        def row_sums(k0, k1, c0, c1, buf):
            nc.vector.tensor_reduce(
                out=pixel_sq[:, k0:k1, c0:c1],
                in_=squares_of(k0, k1, c0, c1, buf).rearrange("p (k w c) -> p k w c", k=k1 - k0, c=64),
                axis=AX.X,
                op=ALU.add,
            )

        def window_sums(k0, k1, z0, z1):
            nc.vector.tensor_tensor(
                out=two_sq[:, k0:k1, z0 : z1 + 2],
                in0=pixel_sq[:, k0:k1, z0 : z1 + 2],
                in1=pixel_sq[:, k0:k1, z0 + 1 : z1 + 3],
                op=ALU.add,
            )
            nc.vector.tensor_tensor(
                out=window_sq[:, k0:k1, z0:z1],
                in0=two_sq[:, k0:k1, z0:z1],
                in1=two_sq[:, k0:k1, z0 + 2 : z1 + 2],
                op=ALU.add,
            )

        def patch_sums_into(sums, half, z0, z1):
            for n, k in enumerate(ROW_TILES_OF[half]):
                nc.tensor.matmul(
                    out=sums[:, 32 * half + z0 : 32 * half + z1],
                    lhsT=gather[:, half, n, :],
                    rhs=window_sq[:, k, z0:z1],
                    start=(n == 0),
                    stop=(n == 1),
                )

        def patch_sums(half, z0, z1):
            sums = psum.tile([P, 64], F32, tag="turned", bufs=3)
            patch_sums_into(sums, half, z0, z1)
            return sums

        def norms_before_root(c0, c1, sums):
            nc.vector.tensor_scalar(
                out=x_norm[:, c0:c1], in0=sums[:, c0:c1], scalar1=1e-12, scalar2=None, op0=ALU.max
            )

        def norms_root(c0, c1):
            nc.scalar.activation(out=x_norm[:, c0:c1], in_=x_norm[:, c0:c1], func=ACT.Sqrt)

        def norms_after_root(c0, c1):
            nc.vector.tensor_scalar(
                out=x_norm[:, c0:c1], in0=x_norm[:, c0:c1], scalar1=qq[:, 0:1], scalar2=None, op0=ALU.add
            )
            nc.vector.reciprocal(out=x_scale[:, c0:c1], in_=x_norm[:, c0:c1])

        live = {}

        def scale(n):
            half, z = n // 32, n % 32
            if n % 4 == 0:
                scaled_new = work.tile([P, 4, 1024], BF16, tag="scaled", bufs=2)
                live[("scaled", n // 4)] = scaled_new
            nc.vector.tensor_scalar(
                out=live[("scaled", n // 4)][:, n % 4, :].rearrange("p (i k) -> p i k", i=4),
                in0=shifted[:, half, :, 64 * z : 64 * z + 256],
                scalar1=x_scale[:, n : n + 1],
                scalar2=None,
                op0=ALU.mult,
            )

        def transposes(n):
            scaled = live[("scaled", n // 4)]
            turned = psum.tile([P, 4, 128], F32, tag="turned", bufs=3)
            for i in range(4):
                nc.tensor.transpose(
                    out=turned[:, i, :], in_=scaled[:, n % 4, 256 * i : 256 * i + 256].bitcast(F32), identity=ident_f[:]
                )
            live[("turned", n)] = turned

        def copy_words(on_scalar, words_out, words_in):
            if on_scalar:
                nc.scalar.copy(out=words_out, in_=words_in)
            else:
                nc.vector.tensor_copy(out=words_out, in_=words_in)

        def leave_psum(n, on_scalar):
            if n % 4 == 0:
                grouped_new = work.tile([P, 4, 1024], BF16, tag="grouped", align_bytes=64)
                live[("grouped", n // 4)] = grouped_new
            grouped = live[("grouped", n // 4)]
            copy_words(
                on_scalar,
                grouped[:, n % 4, :].bitcast(F32).rearrange("p (g n u) -> p g n u", g=2, u=2),
                live[("turned", n)][:].rearrange("p (g u) n -> p g n u", u=2),
            )

        def quantise(n, count):
            if n % 4 == 0:
                codes_new = work.tile([P, 1024], U32, tag="codes", align_bytes=64)
                scales_new = work.tile([P, 1024], U8, tag="scales", align_bytes=64)
                live[("codes", n // 4)] = (codes_new, scales_new)
            codes, scales = live[("codes", n // 4)]
            g0 = n % 4
            nc.vector.quantize_mx(
                out=codes[:, 256 * g0 : 256 * (g0 + count)].bitcast(FP8X4),
                scales=scales[:, 256 * g0 : 256 * (g0 + count)],
                in_=live[("grouped", n // 4)][:, g0 : g0 + count, :].rearrange("p z n -> p (z n)"),
            )

        w_norm = const.tile([P, 4], F32)
        w_scale = const.tile([P, 4], F32)
        unused = epi.tile([P, 1024], BF16, tag="sign", bufs=19)
        w_scaled = work.tile([P, 4, 1024], BF16, tag="scaled", bufs=2)
        w_grouped = work.tile([P, 2, 512, 4], BF16, tag="grouped", align_bytes=64)
        w_words = w_grouped[:].rearrange("p g n t -> p g (n t)").bitcast(F32).rearrange("p g (n u) -> p g n u", u=2)
        w_turned = []
        w_back = []

        def w_transposes(ub):
            w_turned_ub = psum.tile([P, 8, 128], BF16, tag="acc", bufs=4)
            w_turned.append(w_turned_ub)
            for s in range(8):
                nc.tensor.transpose(
                    out=w_turned_ub[:, s, :], in_=w_raw[s // 4][:, s % 4, 128 * ub : 128 * ub + 128], identity=ident_bf[:]
                )

        def w_squares(ub):
            nc.scalar.activation(
                out=unused[:],
                in_=w_turned[ub][:].rearrange("p s k -> p (s k)"),
                func=ACT.Square,
                accum_out=w_norm[:, ub : ub + 1],
            )

        def w_norms(u0, u1):
            cols = slice(u0, u1)
            nc.vector.tensor_scalar(out=w_norm[:, cols], in0=w_norm[:, cols], scalar1=1e-12, scalar2=None, op0=ALU.max)
            nc.scalar.activation(out=w_norm[:, cols], in_=w_norm[:, cols], func=ACT.Sqrt)
            nc.vector.tensor_scalar(
                out=w_norm[:, cols], in0=w_norm[:, cols], scalar1=qq[:, 0:1], scalar2=None, op0=ALU.add
            )
            nc.vector.reciprocal(out=w_scale[:, cols], in_=w_norm[:, cols])

        def w_times_scale(ub, on_scalar):
            w_turned_ub = w_turned[ub][:].rearrange("p s k -> p (s k)")
            factor = w_scale[:, ub : ub + 1]
            if on_scalar:
                nc.scalar.activation(out=w_scaled[:, ub, :], in_=w_turned_ub, func=ACT.Copy, scale=factor)
            else:
                nc.vector.tensor_scalar(
                    out=w_scaled[:, ub, :], in0=w_turned_ub, scalar1=factor, scalar2=None, op0=ALU.mult
                )

        def w_transposes_back(ub):
            w_back_ub = psum.tile([P, 4, 128], F32, tag="acc", bufs=4)
            w_back.append(w_back_ub)
            for i in range(4):
                nc.tensor.transpose(
                    out=w_back_ub[:, i, :], in_=w_scaled[:, ub, 256 * i : 256 * i + 256].bitcast(F32), identity=ident_f[:]
                )

        def w_leave_psum(ub, on_scalar):
            copy_words(on_scalar, w_words[:, :, 128 * ub : 128 * ub + 128, :], w_back[ub][:].rearrange("p (g u) n -> p g n u", u=2))

        expo = psum.tile([P, 512], F32, tag="expo", bufs=1)
        nc.scalar.activation(out=expo_row[0:1, :], in_=p_row[:], func=ACT.Square, scale=0.2)
        nc.tensor.matmul(out=expo[:], lhsT=ones_f[:], rhs=expo_row[:], start=True, stop=True)
        expo_sb = const.tile([P, 512], F32)
        row_squares(0, 2, 0, FIRST_PIXELS, 0)
        row_sums(0, 2, 0, FIRST_PIXELS, 0)
        window_sums(0, 2, 0, FIRST_Z)
        for ub in range(4):
            w_transposes(ub)
        w_squares(0)
        w_squares(1)
        sums_a = patch_sums(0, 0, FIRST_Z)
        norms_before_root(0, FIRST_Z, sums_a)
        norms_root(0, FIRST_Z)
        w_norms(0, 2)
        norms_after_root(0, FIRST_Z)
        w_squares(2)
        w_squares(3)
        w_times_scale(0, False)
        w_times_scale(1, False)
        scale(0)
        scale(1)
        w_transposes_back(0)
        w_transposes_back(1)
        transposes(0)
        transposes(1)
        w_norms(2, 4)
        scale(2)
        scale(3)
        w_leave_psum(0, True)
        w_times_scale(2, False)
        w_times_scale(3, True)
        w_leave_psum(1, False)
        w_transposes_back(2)
        w_transposes_back(3)
        transposes(2)
        leave_psum(0, True)
        leave_psum(1, True)
        w_leave_psum(2, False)
        w_leave_psum(3, True)
        transposes(3)
        leave_psum(2, True)
        quantise(0, 2)
        w_codes = const.tile([P, 1024], U32, align_bytes=64)
        w_scales = const.tile([P, 1024], U8, align_bytes=64)
        nc.vector.quantize_mx(
            out=w_codes[:].bitcast(FP8X4), scales=w_scales[:], in_=w_grouped[:].rearrange("p g n t -> p (g n t)")
        )
        leave_psum(3, True)
        for n in range(4, 8):
            scale(n)
        quantise(2, 2)
        out_v = out.rearrange("b y z u -> (b y) z u")

        def multiply(n):
            codes, scales = live[("codes", n // 4)]
            acc = psum.tile([P, 512], F32, tag="acc", bufs=4)
            for g in range(2):
                c0 = 256 * (n % 4) + 128 * g
                nc.tensor.matmul_mx(
                    out=acc[:],
                    lhsT=codes[:, c0 : c0 + 128].bitcast(FP8X4),
                    lhsT_scale=scales[:, c0 : c0 + 128],
                    rhs=w_codes[:, 512 * g : 512 * g + 512].bitcast(FP8X4),
                    rhs_scale=w_scales[:, 512 * g : 512 * g + 512],
                    start=(g == 0),
                    stop=(g == 1),
                )
            live[("acc", n)] = acc

        def take_sign(n):
            if n % 2 == 0:
                value_new = epi.tile([P, 2, 512], F32, tag="value", bufs=21)
                live[("value", n // 2)] = value_new
            nc.scalar.activation(out=value(n), in_=live[("acc", n)][:], func=ACT.Abs)

        def take_abs(n):
            if n % 2 == 0:
                sign_new = epi.tile([P, 2, 512], BF16, tag="sign", bufs=19)
                live[("sign", n // 2)] = sign_new
            nc.vector.tensor_scalar(
                out=sign(n), in0=live[("acc", n)][:], scalar1=-TINY, scalar2=TINY, op0=ALU.max, op1=ALU.min
            )

        def value(n):
            return live[("value", n // 2)][:, n % 2, :]

        def sign(n):
            return live[("sign", n // 2)][:, n % 2, :]

        def store(n, count):
            half, z = n // 32, n % 32
            nc.sync.dma_start(
                out=out_v[128 * half : 128 * half + 128, z : z + count, :],
                in_=live[("value", n // 2)][:, n % 2 : n % 2 + count, :],
            )

        long_work = []
        start_of = 0
        for c, chunk in enumerate(CHUNKS):
            for ph, func in enumerate((ACT.Ln, ACT.Exp)):
                for n in range(start_of, start_of + chunk, 2):
                    long_work.append((func, n, 2 * c + ph))
            start_of += chunk
        done = {"long": 0, "mult": 0, "sign": 0}
        abs_at, log_at, mult_at, power_at = {}, {}, {}, {}

        def phase():
            return long_work[min(done["long"], len(long_work) - 1)][2]

        def long_piece(step):
            if done["long"] >= len(long_work):
                return
            func, n, ph = long_work[done["long"]]
            v = live.get(("value", n // 2))
            if func == ACT.Ln and step > NORM_END + 1 and abs_at.get(n + 1, step) + LN_LAG <= step:
                nc.scalar.activation(out=v[:], in_=v[:], func=ACT.Ln, bias=eps_t[:, 0:1])
                log_at[n] = step
                log_at[n + 1] = step
                done["long"] += 1
            elif func == ACT.Exp and max(mult_at.get(n, step), mult_at.get(n + 1, step)) + 1 <= step:
                nc.scalar.activation(out=v[:], in_=v[:], func=ACT.Exp, bias=shift_t[:, 0:1])
                power_at[n] = step
                power_at[n + 1] = step
                done["long"] += 1

        def on_gpsimd(m):
            if 2 * m < CHUNKS[0]:
                return spread(m, EXPO_ON_GPSIMD[0])
            return m - CHUNKS[0] // 2 < EXPO_ON_GPSIMD[1]

        def times_exponent(step):
            n = done["mult"]
            if n < GROUPS and log_at.get(n, step) + MULT_LAG <= step:
                if on_gpsimd(n // 2):
                    for k in (n, n + 1):
                        nc.gpsimd.tensor_tensor(out=value(k), in0=value(k), in1=expo_sb[:], op=ALU.mult)
                else:
                    v = live[("value", n // 2)]
                    nc.vector.tensor_tensor(
                        out=v[:], in0=v[:], in1=expo[:].unsqueeze(1).to_broadcast([P, 2, 512]), op=ALU.mult
                    )
                mult_at[n] = step
                mult_at[n + 1] = step
                done["mult"] += 2

        def times_sign(step):
            n = done["sign"]
            if n < GROUPS and power_at.get(n, step) + 1 <= step:
                v, s = live[("value", n // 2)], live[("sign", n // 2)]
                if n < SIGN_ON_GPSIMD:
                    for k in range(2):
                        nc.gpsimd.tensor_tensor(out=v[:, k, :], in0=v[:, k, :], in1=s[:, k, :], op=ALU.mult)
                else:
                    nc.vector.tensor_tensor(out=v[:], in0=v[:], in1=s[:], op=ALU.mult)
                store(n, 2)
                done["sign"] += 2

        for step in range(4 - LEAD, 4 * GROUPS):
            if done["sign"] >= GROUPS:
                break
            drained = step >= GROUPS + 2
            if step == 0:
                nc.vector.tensor_copy(out=expo_sb[:], in_=expo[:])
            for job, (k0, k1, c0, c1, first_step) in enumerate(NORM_JOBS):
                if step == first_step:
                    row_squares(k0, k1, c0, c1, job % 2)
                if step == first_step + 1:
                    row_sums(k0, k1, c0, c1, job % 2)
            if step == NORM_END:
                window_sums(0, 2, FIRST_Z, 32)
                window_sums(2, 3, 0, 32)
            if step == NORM_END + 1:
                live["sums"] = patch_sums(0, FIRST_Z, 32)
                patch_sums_into(live["sums"], 1, 0, 32)
                norms_before_root(FIRST_Z, 64, live["sums"])
                norms_root(FIRST_Z, 64)
            if step == NORM_END + 2:
                norms_after_root(FIRST_Z, 64)
            ahead = step + 1
            if ahead % 4 == 0 and 0 <= ahead < GROUPS:
                if ahead > 0:
                    quantise(ahead, 4)
                if ahead + 8 < GROUPS:
                    for n in range(ahead + 8, ahead + 12):
                        scale(n)
            if 0 <= step < GROUPS:
                multiply(step)
            if 4 <= step + LEAD < GROUPS:
                transposes(step + LEAD)
            if 0 <= step - 1 < GROUPS:
                take_sign(step - 1)
            if 4 <= step + LEAD - 1 < GROUPS:
                leave_psum(step + LEAD - 1, spread(step + LEAD - 1, COPIES_ON_SCALAR[phase()]))
            long_piece(step)
            if 0 <= step - 2 < GROUPS:
                take_abs(step - 2)
                abs_at[step - 2] = step
            for repeat in range(2):
                times_exponent(step)
            for repeat in range(2):
                times_sign(step)
        assert done["sign"] == GROUPS and done["long"] == len(long_work)
